import numpy as np
import ml_dtypes


def mxq(x, axis, fmt="e4m3"):
    dtype, down = {"e4m3": (ml_dtypes.float8_e4m3fn, 7), "e5m2": (ml_dtypes.float8_e5m2, 14)}[fmt]
    v = np.moveaxis(np.asarray(x, np.float32).astype(ml_dtypes.bfloat16).astype(np.float64), axis, -1)
    blocks = v.reshape(v.shape[:-1] + (-1, 32))
    amax = np.abs(blocks).max(-1, keepdims=True)
    byte = np.maximum(np.where(amax > 0, np.frexp(amax)[1] - 1 + 127, 0) - down, 1)
    scale = np.exp2(byte - 127.0)
    codes = (blocks / scale).astype(np.float32).astype(dtype).astype(np.float64)
    return np.moveaxis((codes * scale).reshape(v.shape), -1, axis)


WIDE = False


def mx_kscale(k):
    if not WIDE:
        return np.ones(k)
    levels = np.array([10, -10, 5, -5, 0])
    if k % 512:
        return np.exp2(np.random.permutation(np.resize(levels, k // 32))).repeat(32)
    a = np.empty((k // 512, 16))
    for p in range(k // 512):
        a[p, :8] = np.random.permutation(np.resize(levels, 8))
        for g in range(8):
            far = levels[np.abs(levels - a[p, g]) >= 10]
            a[p, g + 8] = far[np.random.randint(len(far))]
    return np.exp2(a.ravel()).repeat(32)


BF16 = ml_dtypes.bfloat16


def bf(x):
    return np.asarray(x, np.float32).astype(BF16)


def f64(x):
    return np.asarray(x).astype(np.float64)


N, L, WD, C, O = 128, 64, 512, 512, 512
EPS = 1e-8
CONV_CLAMP = 256.0
ACT_GAIN = np.sqrt(2.0)
LRELU_SLOPE = 0.2
STYLE_WSCALE = 1.0 / np.sqrt(WD)
X_AMP = CONV_CLAMP / 2.0
W_AMP = np.sqrt(EPS)


def draw0():
    s, t = mx_kscale(WD), mx_kscale(C)
    return {"x": bf(np.random.standard_normal((N, L, C)) * X_AMP),
            "w": bf(np.random.standard_normal((N, WD)) * s),
            "weight": bf(np.random.standard_normal((O, C)) * W_AMP / np.sqrt(C) / t[None, :]),
            "style_w": bf(np.random.standard_normal((C, WD)) * t[:, None] / s[None, :]),
            "style_b": bf((1.0 + 0.1 * np.random.standard_normal(C)) * t),
            "bias": bf(np.random.standard_normal(O) * 0.2 * X_AMP)}


def core(x, w, weight, style_w, style_b, bias):
    wt = f64(weight)
    style = (mxq(f64(w), 1, "e4m3") @ mxq(f64(style_w), 1, "e4m3").T) * STYLE_WSCALE + f64(style_b)
    d = mxq(np.square(style), 1, "e4m3") @ mxq(np.square(wt), 1, "e4m3").T
    decoef = 1.0 / np.sqrt(d + EPS)
    x_mod = f64(x) * style[:, None, :]
    y = mxq(x_mod, 2, "e4m3") @ mxq(wt, 1, "e4m3").T
    y = y * decoef[:, None, :]
    y = y + f64(bias)
    y = np.where(y >= 0, y, LRELU_SLOPE * y) * ACT_GAIN
    return np.clip(y, -CONV_CLAMP, CONV_CLAMP)


def e4m3fn_bytes(y):
    return np.clip(np.asarray(y, np.float64), -448.0, 448.0).astype(np.float32).astype(ml_dtypes.float8_e4m3fn).view(np.uint8)


def e4m3fn_values(b):
    return np.asarray(b, np.uint8).view(ml_dtypes.float8_e4m3fn).astype(np.float64)


def setup_inputs():
    d = draw0()
    x0 = np.asarray(d['w']).astype(np.float64)
    s = (np.max(np.abs(x0), axis=(0,), keepdims=True) / 448.0).astype(np.float32)
    out = {}
    for k, v in d.items():
        if k == 'w':
            out['w_bytes'] = e4m3fn_bytes(x0 / s.astype(np.float64))
            out['w_scale'] = s
        else:
            out[k] = v
    return out


def reference(x, w_bytes, w_scale, weight, style_w, style_b, bias):
    return core(x, e4m3fn_values(w_bytes) * w_scale.astype(np.float64), weight, style_w, style_b, bias)

@@ -1,0 +1,279 @@
+import math
+from contextlib import ExitStack
+
+import concourse.mybir as mybir
+from concourse.masks import make_identity
+
+N_SAMPLES, L, WD, C, O = 128, 64, 512, 512, 512
+EPS = 1e-8
+CLAMP = 256.0
+SLOPE = 0.2
+GAIN = math.sqrt(2.0)
+FLOPS = 2 * N_SAMPLES * L * C * O + 2 * N_SAMPLES * WD * C + 2 * N_SAMPLES * C * O
+
+F32 = mybir.dt.float32
+BF16 = mybir.dt.bfloat16
+U32 = mybir.dt.uint32
+U8 = mybir.dt.uint8
+FP8 = mybir.dt.float8_e4m3fn
+X4 = mybir.dt.float8_e4m3fn_x4
+ALU = mybir.AluOpType
+ACT = mybir.ActivationFunctionType
+
+P = 128
+T = 4
+NU = 4
+TOK = NU * L
+J = TOK // P
+LG = L // J
+UNITS = N_SAMPLES // NU
+LAG = 2
+
+
+def tile_modulatemlp_pa_kernel(tc, x, w_bytes, w_scale, weight, style_w, style_b, bias, out):
+    nc = tc.nc
+    xv = x.rearrange("n l c -> (n l) c").rearrange("(b p j) c -> b p (j c)", p=P, j=J)
+    ov = out.rearrange("n l o -> (n l) o").rearrange("(b p j) o -> b p (j o)", p=P, j=J)
+
+    with ExitStack() as ctx:
+        ctx.enter_context(tc.manual_schedule())
+        keep = ctx.enter_context(tc.tile_pool(name="keep", bufs=1))
+        xpool = ctx.enter_context(tc.tile_pool(name="xpool", bufs=6))
+        work = ctx.enter_context(tc.tile_pool(name="work", bufs=4))
+        xt_ps = ctx.enter_context(tc.psum_pool(name="xt_ps", bufs=2))
+        y_ps = ctx.enter_context(tc.psum_pool(name="y_ps", bufs=3))
+        z_ps = ctx.enter_context(tc.psum_pool(name="z_ps", bufs=3))
+
+        sw_sb = keep.tile([P, T, WD], BF16)
+        wt_sb = keep.tile([P, T, C], BF16)
+        w8 = keep.tile([P, WD], U8)
+        ws = keep.tile([P, T], F32)
+        sb = keep.tile([P, T], BF16)
+        bs = keep.tile([P, T], BF16)
+        swv = style_w.rearrange("(m t) l -> m t l", t=T)
+        nc.sync.dma_start(out=w8[:], in_=w_bytes)
+        nc.sync.dma_start(out=sw_sb[:, 0:2, :], in_=swv[:, 0:2, :])
+        nc.sync.dma_start(out=sw_sb[:, 2:4, :], in_=swv[:, 2:4, :])
+        nc.scalar.dma_start(out=ws[:], in_=w_scale.rearrange("o (p t) -> p (o t)", t=T))
+        nc.scalar.dma_start(out=sb[:], in_=style_b.rearrange("(p t) -> p t", t=T))
+        nc.scalar.dma_start(out=bs[:], in_=bias.rearrange("(p t) -> p t", t=T))
+        nc.sync.dma_start(out=wt_sb[:], in_=weight.rearrange("(m k) c -> m k c", k=T))
+
+        xs = {}
+
+        def load(i):
+            x_sb = xpool.tile([P, J, C], BF16)
+            nc.sync.dma_start(out=x_sb[:].rearrange("p j c -> p (j c)"), in_=xv[i])
+            xs[i] = x_sb
+
+        for i in range(4):
+            load(i)
+
+        ident = keep.tile([P, P], F32)
+        make_identity(nc, ident[:])
+        warm = keep.tile([P, 1], F32)
+        nc.vector.memset(warm[:], 1.0)
+        warm_out = keep.tile([P, 1], F32)
+        nc.scalar.activation(out=warm_out[:], in_=warm[:], func=ACT.Sqrt)
+
+        def transpose_words(dst, words):
+            for u in range(2):
+                nc.tensor.transpose(dst[:, u, :], words[:, u::2], ident[:])
+
+        w_bf = keep.tile([P, WD], BF16)
+        nc.vector.tensor_copy(out=w_bf[:], in_=w8[:].bitcast(FP8))
+
+        swg = keep.tile([P, T, P, T], BF16, align_bytes=64)
+        sw_t = [y_ps.tile([P, 2, 2, P], F32, name="yt") for h in range(2)]
+        wt_ = xt_ps.tile([P, J, 2, P], F32, name="xt")
+        for h in range(2):
+            for tt in range(2):
+                transpose_words(sw_t[h][:, tt], sw_sb[:, 2 * h + tt, :].bitcast(F32))
+            if h == 0:
+                transpose_words(wt_[:, 0], w_bf[:].bitcast(F32))
+        wg = keep.tile([P, P, T], BF16, align_bytes=64)
+        nc.vector.tensor_copy(
+            out=swg[:, 0:2].rearrange("p t m k -> p t (m k)").bitcast(F32).rearrange("p t (m u) -> p t m u", u=2),
+            in_=sw_t[0][:].rearrange("p t u m -> p t m u"))
+        nc.scalar.copy(
+            out=swg[:, 2:4].rearrange("p t m k -> p t (m k)").bitcast(F32).rearrange("p t (m u) -> p t m u", u=2),
+            in_=sw_t[1][:].rearrange("p t u m -> p t m u"))
+        nc.vector.tensor_tensor(
+            out=wg[:].rearrange("p n (u e) -> p n u e", e=2),
+            in0=wt_[:, 0].bitcast(BF16).rearrange("p u (n e) -> p n u e", e=2),
+            in1=ws[:].rearrange("p (u e) -> p u e", e=2).unsqueeze(1).to_broadcast([P, P, 2, 2]),
+            op=ALU.mult)
+        swq = keep.tile([P, C], U32, align_bytes=64)
+        sws = keep.tile([P, C], U8, align_bytes=64)
+        wq = keep.tile([P, P], U32, align_bytes=64)
+        wqs = keep.tile([P, P], U8, align_bytes=64)
+        nc.vector.quantize_mx(out=swq[:].bitcast(X4), scales=sws[:], in_=swg[:].rearrange("p t m k -> p (t m k)"))
+        nc.vector.quantize_mx(out=wq[:].bitcast(X4), scales=wqs[:], in_=wg[:].rearrange("p n k -> p (n k)"))
+        st_ps = z_ps.tile([P, T, P], F32, name="zt")
+        for t in range(T):
+            cs = slice(t * P, (t + 1) * P)
+            nc.tensor.matmul_mx(out=st_ps[:, t, :], lhsT=swq[:, cs].bitcast(X4), lhsT_scale=sws[:, cs],
+                                rhs=wq[:].bitcast(X4), rhs_scale=wqs[:], start=True, stop=True)
+
+        wtg = keep.tile([P, T, P, T], BF16, align_bytes=64)
+        for h in range(2):
+            wps = y_ps.tile([P, 2, 2, P], F32, name="yt")
+            for kk in range(2):
+                transpose_words(wps[:, kk], wt_sb[:, 2 * h + kk, :].bitcast(F32))
+            nc.scalar.copy(
+                out=wtg[:, 2 * h : 2 * h + 2].rearrange("p t m k -> p t (m k)").bitcast(F32).rearrange("p t (m u) -> p t m u", u=2),
+                in_=wps[:].rearrange("p t u m -> p t m u"))
+        wtf = wtg[:].rearrange("p k m c -> p (k m c)")
+
+        style = keep.tile([P, N_SAMPLES, T], F32)
+        nc.vector.scalar_tensor_tensor(
+            out=style[:], in0=st_ps[:].rearrange("p t n -> p n t"), scalar=1.0 / math.sqrt(WD),
+            in1=sb[:].unsqueeze(1).to_broadcast([P, N_SAMPLES, T]), op0=ALU.mult, op1=ALU.add)
+
+        def transpose_x(i):
+            xt = xt_ps.tile([P, J, 2, P], F32, name="xt")
+            x_sb = xs.pop(i)
+            for j in range(J):
+                transpose_words(xt[:, j], x_sb[:, j, :].bitcast(F32))
+            return xt
+
+        def modulate(i, xt):
+            xm = work.tile([P, J, P, T], BF16, name="xm", align_bytes=64)
+            st = style[:, i * NU : (i + 1) * NU, :].rearrange("p n (u e) -> p n u e", e=2)
+            for j in range(J):
+                nc.vector.tensor_tensor(
+                    out=xm[:, j].rearrange("p (n l) (u e) -> p n l u e", n=NU, e=2),
+                    in0=xt[:, j].bitcast(BF16).rearrange("p u (n l e) -> p n l u e", n=NU, e=2),
+                    in1=st.unsqueeze(2).to_broadcast([P, NU, LG, 2, 2]),
+                    op=ALU.mult)
+            return xm
+
+        def quantize(xm):
+            xq = work.tile([P, TOK], U32, name="xq", align_bytes=64)
+            xqs = work.tile([P, TOK], U8, name="xqs", align_bytes=64)
+            nc.vector.quantize_mx(out=xq[:].bitcast(X4), scales=xqs[:], in_=xm[:].rearrange("p j r t -> p (j r t)"))
+            return xq, xqs
+
+        xts = {0: transpose_x(0)}
+        wtq = keep.tile([P, O], U32, align_bytes=64)
+        wts = keep.tile([P, O], U8, align_bytes=64)
+        nc.vector.quantize_mx(out=wtq[:].bitcast(X4), scales=wts[:], in_=wtf)
+        s2 = keep.tile([P, N_SAMPLES * T], BF16, align_bytes=64)
+        nc.scalar.activation(out=s2[:], in_=style[:].rearrange("p n t -> p (n t)"), func=ACT.Square)
+        w2 = keep.tile([P, O * T], BF16, align_bytes=64)
+        nc.scalar.activation(out=w2[:], in_=wtf, func=ACT.Square)
+        xms = {0: modulate(0, xts.pop(0))}
+        s2q = keep.tile([P, N_SAMPLES], U32, align_bytes=64)
+        s2s = keep.tile([P, N_SAMPLES], U8, align_bytes=64)
+        nc.vector.quantize_mx(out=s2q[:].bitcast(X4), scales=s2s[:], in_=s2[:])
+        xqs_ = {0: quantize(xms.pop(0))}
+        w2q = keep.tile([P, O], U32, align_bytes=64)
+        w2s = keep.tile([P, O], U8, align_bytes=64)
+        nc.vector.quantize_mx(out=w2q[:].bitcast(X4), scales=w2s[:], in_=w2[:])
+        d_ps = z_ps.tile([P, T, P], F32, name="zt")
+        for k in range(T):
+            cs = slice(k * P, (k + 1) * P)
+            nc.tensor.matmul_mx(out=d_ps[:, k, :], lhsT=w2q[:, cs].bitcast(X4), lhsT_scale=w2s[:, cs],
+                                rhs=s2q[:].bitcast(X4), rhs_scale=s2s[:], start=True, stop=True)
+        xts[1] = transpose_x(1)
+        dh = keep.tile([P, T, P], F32)
+        nc.vector.tensor_scalar(out=dh[:], in0=d_ps[:], scalar1=0.5, scalar2=0.5 * EPS, op0=ALU.mult, op1=ALU.add)
+        ds = keep.tile([P, T, P], F32)
+        nc.scalar.activation(out=ds[:], in_=dh[:], func=ACT.Sqrt)
+        dec = keep.tile([P, T, P], F32)
+        nc.vector.reciprocal(out=dec[:], in_=ds[:])
+        bg = keep.tile([P, T], F32)
+        nc.vector.tensor_scalar(out=bg[:], in0=bs[:], scalar1=GAIN, scalar2=None, op0=ALU.mult)
+
+        def affine(i, h, yt, zr):
+            for kk in range(2):
+                k = 2 * h + kk
+                for n in range(NU):
+                    s = i * NU + n
+                    nc.scalar.activation(
+                        out=zr[:, k, :].rearrange("p (j n l) -> p n j l", j=J, n=NU)[:, n],
+                        in_=yt[:, kk, :].rearrange("p (j n l) -> p n j l", j=J, n=NU)[:, n],
+                        func=ACT.Identity, scale=dec[:, k, s : s + 1], bias=bg[:, k : k + 1])
+
+        zcs = {}
+        zrs = {}
+        qs = {}
+
+        def is_sum(i, j):
+            return j == 1
+
+        def finish(i, j, ot):
+            za = zrs[i] if is_sum(i, j) else zcs[i, j]
+            cols = slice(j * P, (j + 1) * P) if is_sum(i, j) else slice(0, P)
+            zt = z_ps.tile([P, T, P], F32, name="zt")
+            summed = is_sum(i, j)
+            for k in range(T):
+                nc.tensor.matmul(out=zt[:, k, :], lhsT=za[:, k, cols], rhs=ident[:], is_transpose=True,
+                                 start=True, stop=not summed)
+                if summed:
+                    nc.tensor.matmul(out=zt[:, k, :], lhsT=qs[i, j][:, k, :], rhs=ident[:], is_transpose=True,
+                                     start=False, stop=True)
+            zv = zt[:].rearrange("p k m -> p m k")
+            o3 = ot[:, j, :].rearrange("p (m k) -> p m k", k=T)
+            if summed:
+                nc.vector.tensor_scalar(out=o3, in0=zv, scalar1=CLAMP, scalar2=-CLAMP, op0=ALU.min, op1=ALU.max)
+            else:
+                qn = work.tile([P, P, T], F32, name="qn")
+                nc.scalar.activation(out=qn[:], in_=zv, func=ACT.Relu, scale=-(1.0 - SLOPE))
+                nc.vector.tensor_tensor(out=o3, in0=zv, in1=qn[:], op=ALU.add)
+
+        def step(i):
+            if i + 4 < UNITS:
+                load(i + 4)
+            if i < UNITS:
+                xq, xqs = xqs_.pop(i)
+                yts = []
+                for h in range(2):
+                    yt = y_ps.tile([P, 2, TOK], F32, name="yt")
+                    for kk in range(2):
+                        cs = slice((2 * h + kk) * P, (2 * h + kk + 1) * P)
+                        nc.tensor.matmul_mx(out=yt[:, kk, :], lhsT=wtq[:, cs].bitcast(X4), lhsT_scale=wts[:, cs],
+                                            rhs=xq[:].bitcast(X4), rhs_scale=xqs[:], start=True, stop=True)
+                    yts.append(yt)
+            if i + 2 < UNITS:
+                xts[i + 2] = transpose_x(i + 2)
+            xm = None
+            if i + 1 < UNITS:
+                xm = modulate(i + 1, xts.pop(i + 1))
+            ot = None
+            if i >= LAG:
+                ot = work.tile([P, J, O], F32, name="ot")
+            if i < UNITS:
+                zr = work.tile([P, T, TOK], F32, name="zr")
+                zrs[i] = zr
+            for h in range(2):
+                if i < UNITS:
+                    affine(i, h, yts[h], zr)
+                if i >= LAG:
+                    finish(i - LAG, h, ot)
+                if h == 0 and xm is not None:
+                    xqs_[i + 1] = quantize(xm)
+            if i < UNITS:
+                for j in range(J):
+                    if is_sum(i, j):
+                        nq = work.tile([P, T, P], F32, name="nq")
+                        nc.gpsimd.tensor_scalar(out=nq[:], in0=zr[:, :, j * P : (j + 1) * P], scalar1=0.0,
+                                                scalar2=-CLAMP / SLOPE, op0=ALU.min, op1=ALU.max)
+                        qs[i, j] = nq
+                for j in range(J):
+                    if not is_sum(i, j):
+                        zc = work.tile([P, T, P], F32, name="zc")
+                        nc.gpsimd.tensor_scalar(out=zc[:], in0=zr[:, :, j * P : (j + 1) * P], scalar1=CLAMP,
+                                                scalar2=-CLAMP / SLOPE, op0=ALU.min, op1=ALU.max)
+                        zcs[i, j] = zc
+                for j in range(J):
+                    if is_sum(i, j):
+                        q = work.tile([P, T, P], F32, name="q")
+                        nc.gpsimd.tensor_scalar(out=q[:], in0=qs[i, j][:], scalar1=-(1.0 - SLOPE),
+                                                scalar2=1.0, op0=ALU.mult, op1=ALU.mult)
+                        qs[i, j] = q
+            if i >= LAG:
+                nc.sync.dma_start(out=ov[i - LAG], in_=ot[:].rearrange("p j o -> p (j o)"))
+
+        for i in range(UNITS + LAG):
+            step(i)

@@ -200,7 +200,7 @@ def tile_modulatemlp_pa_kernel(tc, x, w_bytes, w_scale, weight, style_w, style_b
         qs = {}
 
         def is_sum(i, j):
-            return j == 1
+            return False
 
         def finish(i, j, ot):
             za = zrs[i] if is_sum(i, j) else zcs[i, j]
@@ -230,7 +230,7 @@ def tile_modulatemlp_pa_kernel(tc, x, w_bytes, w_scale, weight, style_w, style_b
                 yts = []
                 for h in range(2):
                     yt = y_ps.tile([P, 2, TOK], F32, name="yt")
-                    for kk in range(2):
+                    for kk in (0, 1, 0, 1):
                         cs = slice((2 * h + kk) * P, (2 * h + kk + 1) * P)
                         nc.tensor.matmul_mx(out=yt[:, kk, :], lhsT=wtq[:, cs].bitcast(X4), lhsT_scale=wts[:, cs],
                                             rhs=xq[:].bitcast(X4), rhs_scale=xqs[:], start=True, stop=True)
@@ -262,7 +262,7 @@ def tile_modulatemlp_pa_kernel(tc, x, w_bytes, w_scale, weight, style_w, style_b
                         qs[i, j] = nq
                 for j in range(J):
                     if not is_sum(i, j):
-                        zc = work.tile([P, T, P], F32, name="zc")
+                        zc = work.tile([P, T, P], F32, name=f"zc{j}")
                         nc.gpsimd.tensor_scalar(out=zc[:], in0=zr[:, :, j * P : (j + 1) * P], scalar1=CLAMP,
                                                 scalar2=-CLAMP / SLOPE, op0=ALU.min, op1=ALU.max)
                         zcs[i, j] = zc

@@ -27,7 +27,12 @@ TOK = NU * L
 J = TOK // P
 LG = L // J
 UNITS = N_SAMPLES // NU
-LAG = 2
+LOADED = 8
+XBUFS = 10
+DUP = (0, 1, 0, 1)
+PIPE = (("L", 8),("M1", 0),("B0", -2),("T", 4),("P0", 3),("Q", 2),("P1", 3),("A0", 0),("R0", -2),("F0", -2),("M0", 1),("B1", -2),("A1", 0),("C0", 0),("C1", 0),("R1", -2),("F1", -2),("ST", -2))
+HEAD_AT = (("square", -3, "T"), ("demod", -3, "P0"), ("recip", -2, "P1"))
+HEAT = (6, 3, 3, 2)
 
 
 def tile_modulatemlp_pa_kernel(tc, x, w_bytes, w_scale, weight, style_w, style_b, bias, out):
@@ -38,7 +43,7 @@ def tile_modulatemlp_pa_kernel(tc, x, w_bytes, w_scale, weight, style_w, style_b
     with ExitStack() as ctx:
         ctx.enter_context(tc.manual_schedule())
         keep = ctx.enter_context(tc.tile_pool(name="keep", bufs=1))
-        xpool = ctx.enter_context(tc.tile_pool(name="xpool", bufs=6))
+        xpool = ctx.enter_context(tc.tile_pool(name="xpool", bufs=XBUFS))
         work = ctx.enter_context(tc.tile_pool(name="work", bufs=4))
         xt_ps = ctx.enter_context(tc.psum_pool(name="xt_ps", bufs=2))
         y_ps = ctx.enter_context(tc.psum_pool(name="y_ps", bufs=3))
@@ -60,220 +65,210 @@ def tile_modulatemlp_pa_kernel(tc, x, w_bytes, w_scale, weight, style_w, style_b
         nc.sync.dma_start(out=wt_sb[:], in_=weight.rearrange("(m k) c -> m k c", k=T))
 
         xs = {}
-
-        def load(i):
-            x_sb = xpool.tile([P, J, C], BF16)
-            nc.sync.dma_start(out=x_sb[:].rearrange("p j c -> p (j c)"), in_=xv[i])
-            xs[i] = x_sb
-
-        for i in range(4):
-            load(i)
+        for u in range(LOADED):
+            x_sb = xpool.tile([P, J, C], BF16, name="x_sb")
+            nc.sync.dma_start(out=x_sb[:].rearrange("p j c -> p (j c)"), in_=xv[u])
+            xs[u] = x_sb
 
         ident = keep.tile([P, P], F32)
         make_identity(nc, ident[:])
-        warm = keep.tile([P, 1], F32)
-        nc.vector.memset(warm[:], 1.0)
+        ones = keep.tile([P, 1], F32)
+        nc.vector.memset(ones[:], 1.0)
         warm_out = keep.tile([P, 1], F32)
-        nc.scalar.activation(out=warm_out[:], in_=warm[:], func=ACT.Sqrt)
+        nc.scalar.activation(out=warm_out[:], in_=ones[:], func=ACT.Sqrt)
+        zero = keep.tile([P, 512], BF16)
+        nc.vector.memset(zero[:], 0.0)
+        eps_half = keep.tile([P, 1], F32)
+        nc.vector.tensor_scalar(out=eps_half[:], in0=ones[:], scalar1=0.5 * EPS, scalar2=None, op0=ALU.mult)
+
+        def heat(count):
+            hot = z_ps.tile([P, 512], F32, name="zt")
+            for r in range(count):
+                nc.tensor.matmul(out=hot[:], lhsT=zero[:, :P], rhs=zero[:], start=True, stop=True)
 
         def transpose_words(dst, words):
             for u in range(2):
                 nc.tensor.transpose(dst[:, u, :], words[:, u::2], ident[:])
 
-        w_bf = keep.tile([P, WD], BF16)
-        nc.vector.tensor_copy(out=w_bf[:], in_=w8[:].bitcast(FP8))
-
+        wtq = keep.tile([P, O], U32, align_bytes=64)
+        wts = keep.tile([P, O], U8, align_bytes=64)
+        s2 = keep.tile([P, N_SAMPLES * T], BF16, align_bytes=64)
+        w2 = keep.tile([P, O * T], BF16, align_bytes=64)
+        s2q = keep.tile([P, N_SAMPLES], U32, align_bytes=64)
+        s2s = keep.tile([P, N_SAMPLES], U8, align_bytes=64)
+        w2q = keep.tile([P, O], U32, align_bytes=64)
+        w2s = keep.tile([P, O], U8, align_bytes=64)
+        ds = keep.tile([P, T, P], F32)
+        dec = keep.tile([P, T, P], F32)
+        bg = keep.tile([P, T], F32)
+        style = keep.tile([P, N_SAMPLES, T], F32)
+        wtg = keep.tile([P, T, P, T], BF16, align_bytes=64)
+        wtf = wtg[:].rearrange("p k m c -> p (k m c)")
         swg = keep.tile([P, T, P, T], BF16, align_bytes=64)
-        sw_t = [y_ps.tile([P, 2, 2, P], F32, name="yt") for h in range(2)]
-        wt_ = xt_ps.tile([P, J, 2, P], F32, name="xt")
-        for h in range(2):
-            for tt in range(2):
-                transpose_words(sw_t[h][:, tt], sw_sb[:, 2 * h + tt, :].bitcast(F32))
-            if h == 0:
-                transpose_words(wt_[:, 0], w_bf[:].bitcast(F32))
         wg = keep.tile([P, P, T], BF16, align_bytes=64)
-        nc.vector.tensor_copy(
-            out=swg[:, 0:2].rearrange("p t m k -> p t (m k)").bitcast(F32).rearrange("p t (m u) -> p t m u", u=2),
-            in_=sw_t[0][:].rearrange("p t u m -> p t m u"))
-        nc.scalar.copy(
-            out=swg[:, 2:4].rearrange("p t m k -> p t (m k)").bitcast(F32).rearrange("p t (m u) -> p t m u", u=2),
-            in_=sw_t[1][:].rearrange("p t u m -> p t m u"))
-        nc.vector.tensor_tensor(
-            out=wg[:].rearrange("p n (u e) -> p n u e", e=2),
-            in0=wt_[:, 0].bitcast(BF16).rearrange("p u (n e) -> p n u e", e=2),
-            in1=ws[:].rearrange("p (u e) -> p u e", e=2).unsqueeze(1).to_broadcast([P, P, 2, 2]),
-            op=ALU.mult)
         swq = keep.tile([P, C], U32, align_bytes=64)
         sws = keep.tile([P, C], U8, align_bytes=64)
         wq = keep.tile([P, P], U32, align_bytes=64)
         wqs = keep.tile([P, P], U8, align_bytes=64)
+
+        def pair(big, h):
+            return big[:, 2 * h : 2 * h + 2].rearrange("p t m k -> p t (m k)").bitcast(F32).rearrange("p t (m u) -> p t m u", u=2)
+
+        heat(HEAT[0])
+        w_bf = keep.tile([P, WD], BF16)
+        nc.vector.tensor_copy(out=w_bf[:], in_=w8[:].bitcast(FP8))
+        sw_t = [y_ps.tile([P, 2, 2, P], F32, name="yt") for h in range(2)]
+        wt_ = y_ps.tile([P, 2, P], F32, name="yt")
+        for h in range(2):
+            for tt in range(2):
+                transpose_words(sw_t[h][:, tt], sw_sb[:, 2 * h + tt, :].bitcast(F32))
+            if h == 0:
+                transpose_words(wt_[:], w_bf[:].bitcast(F32))
+        heat(HEAT[1])
+        nc.vector.tensor_copy(out=pair(swg, 0), in_=sw_t[0][:].rearrange("p t u m -> p t m u"))
+        nc.scalar.copy(out=pair(swg, 1), in_=sw_t[1][:].rearrange("p t u m -> p t m u"))
+        nc.vector.tensor_tensor(
+            out=wg[:].rearrange("p n (u e) -> p n u e", e=2),
+            in0=wt_[:].bitcast(BF16).rearrange("p u (n e) -> p n u e", e=2),
+            in1=ws[:].rearrange("p (u e) -> p u e", e=2).unsqueeze(1).to_broadcast([P, P, 2, 2]),
+            op=ALU.mult)
         nc.vector.quantize_mx(out=swq[:].bitcast(X4), scales=sws[:], in_=swg[:].rearrange("p t m k -> p (t m k)"))
         nc.vector.quantize_mx(out=wq[:].bitcast(X4), scales=wqs[:], in_=wg[:].rearrange("p n k -> p (n k)"))
+        wps = []
+        for h in range(2):
+            w_t = y_ps.tile([P, 2, 2, P], F32, name="yt")
+            for kk in range(2):
+                transpose_words(w_t[:, kk], wt_sb[:, 2 * h + kk, :].bitcast(F32))
+            wps.append(w_t)
+        heat(HEAT[2])
         st_ps = z_ps.tile([P, T, P], F32, name="zt")
         for t in range(T):
             cs = slice(t * P, (t + 1) * P)
             nc.tensor.matmul_mx(out=st_ps[:, t, :], lhsT=swq[:, cs].bitcast(X4), lhsT_scale=sws[:, cs],
                                 rhs=wq[:].bitcast(X4), rhs_scale=wqs[:], start=True, stop=True)
-
-        wtg = keep.tile([P, T, P, T], BF16, align_bytes=64)
         for h in range(2):
-            wps = y_ps.tile([P, 2, 2, P], F32, name="yt")
-            for kk in range(2):
-                transpose_words(wps[:, kk], wt_sb[:, 2 * h + kk, :].bitcast(F32))
-            nc.scalar.copy(
-                out=wtg[:, 2 * h : 2 * h + 2].rearrange("p t m k -> p t (m k)").bitcast(F32).rearrange("p t (m u) -> p t m u", u=2),
-                in_=wps[:].rearrange("p t u m -> p t m u"))
-        wtf = wtg[:].rearrange("p k m c -> p (k m c)")
-
-        style = keep.tile([P, N_SAMPLES, T], F32)
+            nc.scalar.copy(out=pair(wtg, h), in_=wps[h][:].rearrange("p t u m -> p t m u"))
+            half = slice(h * 2 * P * T, (h + 1) * 2 * P * T)
+            nc.vector.tensor_tensor(out=w2[:, half], in0=wtf[:, half], in1=wtf[:, half], op=ALU.mult)
         nc.vector.scalar_tensor_tensor(
             out=style[:], in0=st_ps[:].rearrange("p t n -> p n t"), scalar=1.0 / math.sqrt(WD),
             in1=sb[:].unsqueeze(1).to_broadcast([P, N_SAMPLES, T]), op0=ALU.mult, op1=ALU.add)
 
-        def transpose_x(i):
+        def head_square():
+            nc.scalar.activation(out=s2[:], in_=style[:].rearrange("p n t -> p (n t)"), func=ACT.Square)
+            nc.vector.quantize_mx(out=w2q[:].bitcast(X4), scales=w2s[:], in_=w2[:])
+            nc.vector.quantize_mx(out=wtq[:].bitcast(X4), scales=wts[:], in_=wtf)
+
+        def head_demod():
+            nc.vector.quantize_mx(out=s2q[:].bitcast(X4), scales=s2s[:], in_=s2[:])
+            d_ps = z_ps.tile([P, T, P], F32, name="zt")
+            for k in range(T):
+                cs = slice(k * P, (k + 1) * P)
+                nc.tensor.matmul_mx(out=d_ps[:, k, :], lhsT=w2q[:, cs].bitcast(X4), lhsT_scale=w2s[:, cs],
+                                    rhs=s2q[:].bitcast(X4), rhs_scale=s2s[:], start=True, stop=True)
+            heat(HEAT[3])
+            nc.scalar.activation(out=ds[:], in_=d_ps[:], func=ACT.Sqrt, scale=0.5, bias=eps_half[:])
+
+        def head_recip():
+            nc.vector.reciprocal(out=dec[:], in_=ds[:])
+            nc.vector.tensor_scalar(out=bg[:], in0=bs[:], scalar1=GAIN, scalar2=None, op0=ALU.mult)
+
+        heads = {"square": head_square, "demod": head_demod, "recip": head_recip}
+        codes, raw, mod, yps, zrow, zclip, zt_ps, qneg, outs = {}, {}, {}, {}, {}, {}, {}, {}, {}
+
+        def op_load(u):
+            x_sb = xpool.tile([P, J, C], BF16, name="x_sb")
+            nc.sync.dma_start(out=x_sb[:].rearrange("p j c -> p (j c)"), in_=xv[u])
+            xs[u] = x_sb
+
+        def op_turn(u):
             xt = xt_ps.tile([P, J, 2, P], F32, name="xt")
-            x_sb = xs.pop(i)
+            x_sb = xs.pop(u)
             for j in range(J):
                 transpose_words(xt[:, j], x_sb[:, j, :].bitcast(F32))
-            return xt
+            raw[u] = xt
 
-        def modulate(i, xt):
-            xm = work.tile([P, J, P, T], BF16, name="xm", align_bytes=64)
-            st = style[:, i * NU : (i + 1) * NU, :].rearrange("p n (u e) -> p n u e", e=2)
-            for j in range(J):
-                nc.vector.tensor_tensor(
-                    out=xm[:, j].rearrange("p (n l) (u e) -> p n l u e", n=NU, e=2),
-                    in0=xt[:, j].bitcast(BF16).rearrange("p u (n l e) -> p n l u e", n=NU, e=2),
-                    in1=st.unsqueeze(2).to_broadcast([P, NU, LG, 2, 2]),
-                    op=ALU.mult)
-            return xm
+        def op_mod(u, j):
+            if j == 0:
+                mod[u] = work.tile([P, J, P, T], BF16, name="xm", align_bytes=64)
+            st = style[:, u * NU : (u + 1) * NU, :].rearrange("p n (u e) -> p n u e", e=2)
+            nc.vector.tensor_tensor(
+                out=mod[u][:, j].rearrange("p (n l) (u e) -> p n l u e", n=NU, e=2),
+                in0=raw[u][:, j].bitcast(BF16).rearrange("p u (n l e) -> p n l u e", n=NU, e=2),
+                in1=st.unsqueeze(2).to_broadcast([P, NU, LG, 2, 2]),
+                op=ALU.mult)
 
-        def quantize(xm):
+        def op_quant(u):
             xq = work.tile([P, TOK], U32, name="xq", align_bytes=64)
             xqs = work.tile([P, TOK], U8, name="xqs", align_bytes=64)
-            nc.vector.quantize_mx(out=xq[:].bitcast(X4), scales=xqs[:], in_=xm[:].rearrange("p j r t -> p (j r t)"))
-            return xq, xqs
+            nc.vector.quantize_mx(out=xq[:].bitcast(X4), scales=xqs[:],
+                                  in_=mod.pop(u)[:].rearrange("p j r t -> p (j r t)"))
+            codes[u] = (xq, xqs)
 
-        xts = {0: transpose_x(0)}
-        wtq = keep.tile([P, O], U32, align_bytes=64)
-        wts = keep.tile([P, O], U8, align_bytes=64)
-        nc.vector.quantize_mx(out=wtq[:].bitcast(X4), scales=wts[:], in_=wtf)
-        s2 = keep.tile([P, N_SAMPLES * T], BF16, align_bytes=64)
-        nc.scalar.activation(out=s2[:], in_=style[:].rearrange("p n t -> p (n t)"), func=ACT.Square)
-        w2 = keep.tile([P, O * T], BF16, align_bytes=64)
-        nc.scalar.activation(out=w2[:], in_=wtf, func=ACT.Square)
-        xms = {0: modulate(0, xts.pop(0))}
-        s2q = keep.tile([P, N_SAMPLES], U32, align_bytes=64)
-        s2s = keep.tile([P, N_SAMPLES], U8, align_bytes=64)
-        nc.vector.quantize_mx(out=s2q[:].bitcast(X4), scales=s2s[:], in_=s2[:])
-        xqs_ = {0: quantize(xms.pop(0))}
-        w2q = keep.tile([P, O], U32, align_bytes=64)
-        w2s = keep.tile([P, O], U8, align_bytes=64)
-        nc.vector.quantize_mx(out=w2q[:].bitcast(X4), scales=w2s[:], in_=w2[:])
-        d_ps = z_ps.tile([P, T, P], F32, name="zt")
-        for k in range(T):
-            cs = slice(k * P, (k + 1) * P)
-            nc.tensor.matmul_mx(out=d_ps[:, k, :], lhsT=w2q[:, cs].bitcast(X4), lhsT_scale=w2s[:, cs],
-                                rhs=s2q[:].bitcast(X4), rhs_scale=s2s[:], start=True, stop=True)
-        xts[1] = transpose_x(1)
-        dh = keep.tile([P, T, P], F32)
-        nc.vector.tensor_scalar(out=dh[:], in0=d_ps[:], scalar1=0.5, scalar2=0.5 * EPS, op0=ALU.mult, op1=ALU.add)
-        ds = keep.tile([P, T, P], F32)
-        nc.scalar.activation(out=ds[:], in_=dh[:], func=ACT.Sqrt)
-        dec = keep.tile([P, T, P], F32)
-        nc.vector.reciprocal(out=dec[:], in_=ds[:])
-        bg = keep.tile([P, T], F32)
-        nc.vector.tensor_scalar(out=bg[:], in0=bs[:], scalar1=GAIN, scalar2=None, op0=ALU.mult)
+        def op_mm(u, h):
+            xq, xqs = codes[u]
+            yt = y_ps.tile([P, 2, TOK], F32, name="yt")
+            for kk in DUP:
+                cs = slice((2 * h + kk) * P, (2 * h + kk + 1) * P)
+                nc.tensor.matmul_mx(out=yt[:, kk, :], lhsT=wtq[:, cs].bitcast(X4), lhsT_scale=wts[:, cs],
+                                    rhs=xq[:].bitcast(X4), rhs_scale=xqs[:], start=True, stop=True)
+            yps[u, h] = yt
 
-        def affine(i, h, yt, zr):
+        def op_affine(u, h):
+            if h == 0:
+                zrow[u] = work.tile([P, T, TOK], F32, name="zr")
+            yt = yps.pop((u, h))
             for kk in range(2):
                 k = 2 * h + kk
                 for n in range(NU):
-                    s = i * NU + n
+                    s = u * NU + n
                     nc.scalar.activation(
-                        out=zr[:, k, :].rearrange("p (j n l) -> p n j l", j=J, n=NU)[:, n],
+                        out=zrow[u][:, k, :].rearrange("p (j n l) -> p n j l", j=J, n=NU)[:, n],
                         in_=yt[:, kk, :].rearrange("p (j n l) -> p n j l", j=J, n=NU)[:, n],
                         func=ACT.Identity, scale=dec[:, k, s : s + 1], bias=bg[:, k : k + 1])
 
-        zcs = {}
-        zrs = {}
-        qs = {}
+        def op_clip(u, h):
+            if h == 0:
+                zclip[u] = work.tile([P, T, TOK], F32, name="zc")
+            ks = slice(2 * h, 2 * h + 2)
+            nc.gpsimd.tensor_scalar(out=zclip[u][:, ks, :], in0=zrow[u][:, ks, :], scalar1=CLAMP,
+                                    scalar2=-CLAMP / SLOPE, op0=ALU.min, op1=ALU.max)
 
-        def is_sum(i, j):
-            return False
-
-        def finish(i, j, ot):
-            za = zrs[i] if is_sum(i, j) else zcs[i, j]
-            cols = slice(j * P, (j + 1) * P) if is_sum(i, j) else slice(0, P)
+        def op_back(u, j):
             zt = z_ps.tile([P, T, P], F32, name="zt")
-            summed = is_sum(i, j)
             for k in range(T):
-                nc.tensor.matmul(out=zt[:, k, :], lhsT=za[:, k, cols], rhs=ident[:], is_transpose=True,
-                                 start=True, stop=not summed)
-                if summed:
-                    nc.tensor.matmul(out=zt[:, k, :], lhsT=qs[i, j][:, k, :], rhs=ident[:], is_transpose=True,
-                                     start=False, stop=True)
-            zv = zt[:].rearrange("p k m -> p m k")
-            o3 = ot[:, j, :].rearrange("p (m k) -> p m k", k=T)
-            if summed:
-                nc.vector.tensor_scalar(out=o3, in0=zv, scalar1=CLAMP, scalar2=-CLAMP, op0=ALU.min, op1=ALU.max)
-            else:
-                qn = work.tile([P, P, T], F32, name="qn")
-                nc.scalar.activation(out=qn[:], in_=zv, func=ACT.Relu, scale=-(1.0 - SLOPE))
-                nc.vector.tensor_tensor(out=o3, in0=zv, in1=qn[:], op=ALU.add)
+                nc.tensor.transpose(zt[:, k, :], zclip[u][:, k, j * P : (j + 1) * P], ident[:])
+            zt_ps[u, j] = zt
 
-        def step(i):
-            if i + 4 < UNITS:
-                load(i + 4)
-            if i < UNITS:
-                xq, xqs = xqs_.pop(i)
-                yts = []
-                for h in range(2):
-                    yt = y_ps.tile([P, 2, TOK], F32, name="yt")
-                    for kk in (0, 1, 0, 1):
-                        cs = slice((2 * h + kk) * P, (2 * h + kk + 1) * P)
-                        nc.tensor.matmul_mx(out=yt[:, kk, :], lhsT=wtq[:, cs].bitcast(X4), lhsT_scale=wts[:, cs],
-                                            rhs=xq[:].bitcast(X4), rhs_scale=xqs[:], start=True, stop=True)
-                    yts.append(yt)
-            if i + 2 < UNITS:
-                xts[i + 2] = transpose_x(i + 2)
-            xm = None
-            if i + 1 < UNITS:
-                xm = modulate(i + 1, xts.pop(i + 1))
-            ot = None
-            if i >= LAG:
-                ot = work.tile([P, J, O], F32, name="ot")
-            if i < UNITS:
-                zr = work.tile([P, T, TOK], F32, name="zr")
-                zrs[i] = zr
-            for h in range(2):
-                if i < UNITS:
-                    affine(i, h, yts[h], zr)
-                if i >= LAG:
-                    finish(i - LAG, h, ot)
-                if h == 0 and xm is not None:
-                    xqs_[i + 1] = quantize(xm)
-            if i < UNITS:
-                for j in range(J):
-                    if is_sum(i, j):
-                        nq = work.tile([P, T, P], F32, name="nq")
-                        nc.gpsimd.tensor_scalar(out=nq[:], in0=zr[:, :, j * P : (j + 1) * P], scalar1=0.0,
-                                                scalar2=-CLAMP / SLOPE, op0=ALU.min, op1=ALU.max)
-                        qs[i, j] = nq
-                for j in range(J):
-                    if not is_sum(i, j):
-                        zc = work.tile([P, T, P], F32, name=f"zc{j}")
-                        nc.gpsimd.tensor_scalar(out=zc[:], in0=zr[:, :, j * P : (j + 1) * P], scalar1=CLAMP,
-                                                scalar2=-CLAMP / SLOPE, op0=ALU.min, op1=ALU.max)
-                        zcs[i, j] = zc
-                for j in range(J):
-                    if is_sum(i, j):
-                        q = work.tile([P, T, P], F32, name="q")
-                        nc.gpsimd.tensor_scalar(out=q[:], in0=qs[i, j][:], scalar1=-(1.0 - SLOPE),
-                                                scalar2=1.0, op0=ALU.mult, op1=ALU.mult)
-                        qs[i, j] = q
-            if i >= LAG:
-                nc.sync.dma_start(out=ov[i - LAG], in_=ot[:].rearrange("p j o -> p (j o)"))
+        def op_neg(u, j):
+            qn = work.tile([P, P, T], F32, name="qn")
+            nc.scalar.activation(out=qn[:], in_=zt_ps[u, j][:].rearrange("p k m -> p m k"), func=ACT.Relu,
+                                 scale=-(1.0 - SLOPE))
+            qneg[u, j] = qn
 
-        for i in range(UNITS + LAG):
-            step(i)
+        def op_out(u, j):
+            if j == 0:
+                outs[u] = work.tile([P, J, O], F32, name="ot")
+            nc.vector.tensor_tensor(out=outs[u][:, j, :].rearrange("p (m k) -> p m k", k=T),
+                                    in0=zt_ps[u, j][:].rearrange("p k m -> p m k"), in1=qneg[u, j][:], op=ALU.add)
+
+        def op_store(u):
+            nc.sync.dma_start(out=ov[u], in_=outs[u][:].rearrange("p j o -> p (j o)"))
+
+        ops = {"L": op_load, "T": op_turn, "Q": op_quant, "ST": op_store,
+               "P0": lambda u: op_mod(u, 0), "P1": lambda u: op_mod(u, 1),
+               "M0": lambda u: op_mm(u, 0), "M1": lambda u: op_mm(u, 1),
+               "A0": lambda u: op_affine(u, 0), "A1": lambda u: op_affine(u, 1),
+               "C0": lambda u: op_clip(u, 0), "C1": lambda u: op_clip(u, 1),
+               "B0": lambda u: op_back(u, 0), "B1": lambda u: op_back(u, 1),
+               "R0": lambda u: op_neg(u, 0), "R1": lambda u: op_neg(u, 1),
+               "F0": lambda u: op_out(u, 0), "F1": lambda u: op_out(u, 1)}
+        first = -max(o for name, o in PIPE if name != "L")
+        for i in range(first, UNITS + 8):
+            for name, o in PIPE:
+                for what, hi, hname in HEAD_AT:
+                    if (i, name) == (hi, hname):
+                        heads[what]()
+                u = i + o
+                if 0 <= u < UNITS and not (name == "L" and u < LOADED):
+                    ops[name](u)

@@ -4,12 +4,12 @@ from contextlib import ExitStack
 import concourse.mybir as mybir
 from concourse.masks import make_identity
 
-N_SAMPLES, L, WD, C, O = 128, 64, 512, 512, 512
+SAMPLES, POINTS, LATENT, C, O = 128, 64, 512, 512, 512
 EPS = 1e-8
 CLAMP = 256.0
 SLOPE = 0.2
 GAIN = math.sqrt(2.0)
-FLOPS = 2 * N_SAMPLES * L * C * O + 2 * N_SAMPLES * WD * C + 2 * N_SAMPLES * C * O
+FLOPS = 2 * SAMPLES * POINTS * C * O + 2 * SAMPLES * LATENT * C + 2 * SAMPLES * C * O
 
 F32 = mybir.dt.float32
 BF16 = mybir.dt.bfloat16
@@ -21,254 +21,366 @@ ALU = mybir.AluOpType
 ACT = mybir.ActivationFunctionType
 
 P = 128
-T = 4
-NU = 4
-TOK = NU * L
-J = TOK // P
-LG = L // J
-UNITS = N_SAMPLES // NU
-LOADED = 8
-XBUFS = 10
-DUP = (0, 1, 0, 1)
-PIPE = (("L", 8),("M1", 0),("B0", -2),("T", 4),("P0", 3),("Q", 2),("P1", 3),("A0", 0),("R0", -2),("F0", -2),("M0", 1),("B1", -2),("A1", 0),("C0", 0),("C1", 0),("R1", -2),("F1", -2),("ST", -2))
-HEAD_AT = (("square", -3, "T"), ("demod", -3, "P0"), ("recip", -2, "P1"))
-HEAT = (6, 3, 3, 2)
+PACK = 4
+GROUP_SAMPLES = 4
+TOKENS = GROUP_SAMPLES * POINTS
+J = TOKENS // P
+ROWS = POINTS // J
+GROUPS = SAMPLES // GROUP_SAMPLES
+HALF = SAMPLES // 2
+PRELOADED = 8
+X_TILES = PRELOADED + 2
+
+SUMMED = {(u, 1) for u in range(0, GROUPS - 2, 2)} | {(GROUPS - 3, 1)}
+VECTOR_RELU = {(GROUPS - 3, 0)}
+
+IDENTITY_PRODUCT = (0, PACK - 1)
+IDENTITY_PRODUCT_GROUPS = GROUPS - 2
+
+STEPS = (
+    ("load", PRELOADED),
+    ("back 0", -2),
+    ("modulate 0", 3),
+    ("demodulate 0", 0),
+    ("quantise", 2),
+    ("product 1", 0),
+    ("relu 0", -2),
+    ("demodulate 1", 0),
+    ("clip 0", 0),
+    ("finish 0", -2),
+    ("product 0", 1),
+    ("clip 1", 0),
+    ("back 1", -2),
+    ("steep", 0),
+    ("relu 1", -2),
+    ("modulate 1", 3),
+    ("turn", 4),
+    ("finish 1", -2),
+    ("store", -2),
+)
+FIRST_TURN = -4
+EARLY = {("turn", 0), ("turn", 1), ("modulate 0", 0), ("modulate 0", 1)} | {("load", u) for u in range(PRELOADED)}
+SECOND_HALF = {
+    (-2, "quantise"): "style",
+    (-2, "steep"): "square",
+    (-1, "product 1"): "quantise",
+    (0, "back 1"): "product",
+    (2, "clip 0"): "root",
+    (3, "steep"): "reciprocal",
+}
 
 
 def tile_modulatemlp_pa_kernel(tc, x, w_bytes, w_scale, weight, style_w, style_b, bias, out):
     nc = tc.nc
-    xv = x.rearrange("n l c -> (n l) c").rearrange("(b p j) c -> b p (j c)", p=P, j=J)
-    ov = out.rearrange("n l o -> (n l) o").rearrange("(b p j) o -> b p (j o)", p=P, j=J)
+    x_view = x.rearrange("n l c -> (n l) c").rearrange("(g r j) c -> g r (j c)", r=P, j=J)
+    out_view = out.rearrange("n l o -> (n l) o").rearrange("(g r j) o -> g r (j o)", r=P, j=J)
 
     with ExitStack() as ctx:
         ctx.enter_context(tc.manual_schedule())
         keep = ctx.enter_context(tc.tile_pool(name="keep", bufs=1))
-        xpool = ctx.enter_context(tc.tile_pool(name="xpool", bufs=XBUFS))
+        x_pool = ctx.enter_context(tc.tile_pool(name="x_pool", bufs=X_TILES))
         work = ctx.enter_context(tc.tile_pool(name="work", bufs=4))
         xt_ps = ctx.enter_context(tc.psum_pool(name="xt_ps", bufs=2))
         y_ps = ctx.enter_context(tc.psum_pool(name="y_ps", bufs=3))
         z_ps = ctx.enter_context(tc.psum_pool(name="z_ps", bufs=3))
 
-        sw_sb = keep.tile([P, T, WD], BF16)
-        wt_sb = keep.tile([P, T, C], BF16)
-        w8 = keep.tile([P, WD], U8)
-        ws = keep.tile([P, T], F32)
-        sb = keep.tile([P, T], BF16)
-        bs = keep.tile([P, T], BF16)
-        swv = style_w.rearrange("(m t) l -> m t l", t=T)
-        nc.sync.dma_start(out=w8[:], in_=w_bytes)
-        nc.sync.dma_start(out=sw_sb[:, 0:2, :], in_=swv[:, 0:2, :])
-        nc.sync.dma_start(out=sw_sb[:, 2:4, :], in_=swv[:, 2:4, :])
-        nc.scalar.dma_start(out=ws[:], in_=w_scale.rearrange("o (p t) -> p (o t)", t=T))
-        nc.scalar.dma_start(out=sb[:], in_=style_b.rearrange("(p t) -> p t", t=T))
-        nc.scalar.dma_start(out=bs[:], in_=bias.rearrange("(p t) -> p t", t=T))
-        nc.sync.dma_start(out=wt_sb[:], in_=weight.rearrange("(m k) c -> m k c", k=T))
+        style_w_sb = keep.tile([P, PACK, LATENT], BF16)
+        weight_sb = keep.tile([P, PACK, C], BF16)
+        w_codes = keep.tile([P, LATENT], U8)
+        w_scale_sb = keep.tile([P, PACK], F32)
+        style_b_sb = keep.tile([P, PACK], BF16)
+        bias_sb = keep.tile([P, PACK], BF16)
+        style_w_view = style_w.rearrange("(m t) l -> m t l", t=PACK)
+        nc.sync.dma_start(out=w_codes[:], in_=w_bytes)
+        nc.sync.dma_start(out=style_w_sb[:, 0:2, :], in_=style_w_view[:, 0:2, :])
+        nc.sync.dma_start(out=style_w_sb[:, 2:4, :], in_=style_w_view[:, 2:4, :])
+        nc.scalar.dma_start(out=w_scale_sb[:], in_=w_scale.rearrange("o (p t) -> p (o t)", t=PACK))
+        nc.scalar.dma_start(out=style_b_sb[:], in_=style_b.rearrange("(p t) -> p t", t=PACK))
+        nc.scalar.dma_start(out=bias_sb[:], in_=bias.rearrange("(p t) -> p t", t=PACK))
+        nc.sync.dma_start(out=weight_sb[:], in_=weight.rearrange("(m k) c -> m k c", k=PACK))
 
-        xs = {}
-        for u in range(LOADED):
-            x_sb = xpool.tile([P, J, C], BF16, name="x_sb")
-            nc.sync.dma_start(out=x_sb[:].rearrange("p j c -> p (j c)"), in_=xv[u])
-            xs[u] = x_sb
+        x_tiles = {}
+
+        def load(u):
+            x_sb = x_pool.tile([P, J, C], BF16, name="x_sb")
+            nc.sync.dma_start(out=x_sb[:].rearrange("p j c -> p (j c)"), in_=x_view[u])
+            x_tiles[u] = x_sb
+
+        for u in range(PRELOADED):
+            load(u)
 
         ident = keep.tile([P, P], F32)
         make_identity(nc, ident[:])
         ones = keep.tile([P, 1], F32)
         nc.vector.memset(ones[:], 1.0)
-        warm_out = keep.tile([P, 1], F32)
-        nc.scalar.activation(out=warm_out[:], in_=ones[:], func=ACT.Sqrt)
+        table_out = keep.tile([P, 1], F32)
+        nc.scalar.activation(out=table_out[:], in_=ones[:], func=ACT.Sqrt)
         zero = keep.tile([P, 512], BF16)
         nc.vector.memset(zero[:], 0.0)
-        eps_half = keep.tile([P, 1], F32)
-        nc.vector.tensor_scalar(out=eps_half[:], in0=ones[:], scalar1=0.5 * EPS, scalar2=None, op0=ALU.mult)
+        half_eps = keep.tile([P, 1], F32)
+        nc.vector.tensor_scalar(out=half_eps[:], in0=ones[:], scalar1=0.5 * EPS, scalar2=None, op0=ALU.mult)
 
-        def heat(count):
-            hot = z_ps.tile([P, 512], F32, name="zt")
+        style_w_q = keep.tile([P, C], U32, align_bytes=64)
+        style_w_s = keep.tile([P, C], U8, align_bytes=64)
+        w_q = keep.tile([P, SAMPLES], U32, align_bytes=64)
+        w_s = keep.tile([P, SAMPLES], U8, align_bytes=64)
+        weight_q = keep.tile([P, O], U32, align_bytes=64)
+        weight_s = keep.tile([P, O], U8, align_bytes=64)
+        weight2_q = keep.tile([P, O], U32, align_bytes=64)
+        weight2_s = keep.tile([P, O], U8, align_bytes=64)
+        style2_q = keep.tile([P, SAMPLES], U32, align_bytes=64)
+        style2_s = keep.tile([P, SAMPLES], U8, align_bytes=64)
+        style_w_t = keep.tile([P, PACK, P, PACK], BF16, align_bytes=64)
+        w_t = keep.tile([P, SAMPLES, PACK], BF16, align_bytes=64)
+        weight_t = keep.tile([P, PACK, P, PACK], BF16, align_bytes=64)
+        weight2_t = keep.tile([P, O * PACK], BF16, align_bytes=64)
+        style2_t = keep.tile([P, SAMPLES * PACK], BF16, align_bytes=64)
+        weight_flat = weight_t[:].rearrange("p k m c -> p (k m c)")
+        w_bf = keep.tile([P, LATENT], BF16)
+        style = keep.tile([P, SAMPLES, PACK], F32)
+        root = keep.tile([P, PACK, SAMPLES], F32)
+        decoef = keep.tile([P, PACK, SAMPLES], F32)
+        bias_gain = keep.tile([P, PACK], F32)
+
+        def transpose_words(dst, row):
+            words = row.bitcast(F32)
+            for h in range(2):
+                nc.tensor.transpose(dst[:, h, :], words[:, h::2], ident[:])
+
+        def halves(big, h):
+            part = big[:, 2 * h : 2 * h + 2].rearrange("p t m k -> p t (m k)").bitcast(F32)
+            return part.rearrange("p t (m u) -> p t m u", u=2)
+
+        def warm(count):
+            unused = xt_ps.tile([P, J, 2, P], F32, name="xt")
             for r in range(count):
-                nc.tensor.matmul(out=hot[:], lhsT=zero[:, :P], rhs=zero[:], start=True, stop=True)
+                nc.tensor.matmul(out=unused[:].rearrange("p j u r -> p (j u r)"), lhsT=zero[:, :P], rhs=zero[:],
+                                 start=True, stop=True)
 
-        def transpose_words(dst, words):
-            for u in range(2):
-                nc.tensor.transpose(dst[:, u, :], words[:, u::2], ident[:])
+        def warm_mx(count):
+            unused = y_ps.tile([P, 2, TOKENS], F32, name="yt")
+            for r in range(count):
+                nc.tensor.matmul_mx(out=unused[:].rearrange("p j u -> p (j u)"), lhsT=style_w_q[:, :P].bitcast(X4),
+                                    lhsT_scale=style_w_s[:, :P], rhs=style_w_q[:].bitcast(X4),
+                                    rhs_scale=style_w_s[:], start=True, stop=True)
 
-        wtq = keep.tile([P, O], U32, align_bytes=64)
-        wts = keep.tile([P, O], U8, align_bytes=64)
-        s2 = keep.tile([P, N_SAMPLES * T], BF16, align_bytes=64)
-        w2 = keep.tile([P, O * T], BF16, align_bytes=64)
-        s2q = keep.tile([P, N_SAMPLES], U32, align_bytes=64)
-        s2s = keep.tile([P, N_SAMPLES], U8, align_bytes=64)
-        w2q = keep.tile([P, O], U32, align_bytes=64)
-        w2s = keep.tile([P, O], U8, align_bytes=64)
-        ds = keep.tile([P, T, P], F32)
-        dec = keep.tile([P, T, P], F32)
-        bg = keep.tile([P, T], F32)
-        style = keep.tile([P, N_SAMPLES, T], F32)
-        wtg = keep.tile([P, T, P, T], BF16, align_bytes=64)
-        wtf = wtg[:].rearrange("p k m c -> p (k m c)")
-        swg = keep.tile([P, T, P, T], BF16, align_bytes=64)
-        wg = keep.tile([P, P, T], BF16, align_bytes=64)
-        swq = keep.tile([P, C], U32, align_bytes=64)
-        sws = keep.tile([P, C], U8, align_bytes=64)
-        wq = keep.tile([P, P], U32, align_bytes=64)
-        wqs = keep.tile([P, P], U8, align_bytes=64)
+        def turn_rows(pool, name, rows, h):
+            turned = pool.tile([P, 2, 2, P], F32, name=name)
+            for k in range(2):
+                transpose_words(turned[:, k], rows[:, 2 * h + k, :])
+            return turned
 
-        def pair(big, h):
-            return big[:, 2 * h : 2 * h + 2].rearrange("p t m k -> p t (m k)").bitcast(F32).rearrange("p t (m u) -> p t m u", u=2)
+        def quantise_style_w(h):
+            cols = slice(2 * P * h, 2 * P * (h + 1))
+            nc.vector.quantize_mx(out=style_w_q[:, cols].bitcast(X4), scales=style_w_s[:, cols],
+                                  in_=style_w_t[:, 2 * h : 2 * h + 2].rearrange("p t m k -> p (t m k)"))
 
-        heat(HEAT[0])
-        w_bf = keep.tile([P, WD], BF16)
-        nc.vector.tensor_copy(out=w_bf[:], in_=w8[:].bitcast(FP8))
-        sw_t = [y_ps.tile([P, 2, 2, P], F32, name="yt") for h in range(2)]
-        wt_ = y_ps.tile([P, 2, P], F32, name="yt")
-        for h in range(2):
-            for tt in range(2):
-                transpose_words(sw_t[h][:, tt], sw_sb[:, 2 * h + tt, :].bitcast(F32))
-            if h == 0:
-                transpose_words(wt_[:], w_bf[:].bitcast(F32))
-        heat(HEAT[1])
-        nc.vector.tensor_copy(out=pair(swg, 0), in_=sw_t[0][:].rearrange("p t u m -> p t m u"))
-        nc.scalar.copy(out=pair(swg, 1), in_=sw_t[1][:].rearrange("p t u m -> p t m u"))
-        nc.vector.tensor_tensor(
-            out=wg[:].rearrange("p n (u e) -> p n u e", e=2),
-            in0=wt_[:].bitcast(BF16).rearrange("p u (n e) -> p n u e", e=2),
-            in1=ws[:].rearrange("p (u e) -> p u e", e=2).unsqueeze(1).to_broadcast([P, P, 2, 2]),
-            op=ALU.mult)
-        nc.vector.quantize_mx(out=swq[:].bitcast(X4), scales=sws[:], in_=swg[:].rearrange("p t m k -> p (t m k)"))
-        nc.vector.quantize_mx(out=wq[:].bitcast(X4), scales=wqs[:], in_=wg[:].rearrange("p n k -> p (n k)"))
-        wps = []
-        for h in range(2):
-            w_t = y_ps.tile([P, 2, 2, P], F32, name="yt")
-            for kk in range(2):
-                transpose_words(w_t[:, kk], wt_sb[:, 2 * h + kk, :].bitcast(F32))
-            wps.append(w_t)
-        heat(HEAT[2])
-        st_ps = z_ps.tile([P, T, P], F32, name="zt")
-        for t in range(T):
-            cs = slice(t * P, (t + 1) * P)
-            nc.tensor.matmul_mx(out=st_ps[:, t, :], lhsT=swq[:, cs].bitcast(X4), lhsT_scale=sws[:, cs],
-                                rhs=wq[:].bitcast(X4), rhs_scale=wqs[:], start=True, stop=True)
-        for h in range(2):
-            nc.scalar.copy(out=pair(wtg, h), in_=wps[h][:].rearrange("p t u m -> p t m u"))
-            half = slice(h * 2 * P * T, (h + 1) * 2 * P * T)
-            nc.vector.tensor_tensor(out=w2[:, half], in0=wtf[:, half], in1=wtf[:, half], op=ALU.mult)
-        nc.vector.scalar_tensor_tensor(
-            out=style[:], in0=st_ps[:].rearrange("p t n -> p n t"), scalar=1.0 / math.sqrt(WD),
-            in1=sb[:].unsqueeze(1).to_broadcast([P, N_SAMPLES, T]), op0=ALU.mult, op1=ALU.add)
+        def square_on_scalar(h):
+            cols = slice(h * 2 * P * PACK, (h + 1) * 2 * P * PACK)
+            nc.scalar.activation(out=weight2_t[:, cols], in_=weight_flat[:, cols], func=ACT.Square)
 
-        def head_square():
-            nc.scalar.activation(out=s2[:], in_=style[:].rearrange("p n t -> p (n t)"), func=ACT.Square)
-            nc.vector.quantize_mx(out=w2q[:].bitcast(X4), scales=w2s[:], in_=w2[:])
-            nc.vector.quantize_mx(out=wtq[:].bitcast(X4), scales=wts[:], in_=wtf)
+        def square_on_vector(h):
+            cols = slice(h * 2 * P * PACK, (h + 1) * 2 * P * PACK)
+            nc.vector.tensor_tensor(out=weight2_t[:, cols], in0=weight_flat[:, cols], in1=weight_flat[:, cols], op=ALU.mult)
 
-        def head_demod():
-            nc.vector.quantize_mx(out=s2q[:].bitcast(X4), scales=s2s[:], in_=s2[:])
-            d_ps = z_ps.tile([P, T, P], F32, name="zt")
-            for k in range(T):
-                cs = slice(k * P, (k + 1) * P)
-                nc.tensor.matmul_mx(out=d_ps[:, k, :], lhsT=w2q[:, cs].bitcast(X4), lhsT_scale=w2s[:, cs],
-                                    rhs=s2q[:].bitcast(X4), rhs_scale=s2s[:], start=True, stop=True)
-            heat(HEAT[3])
-            nc.scalar.activation(out=ds[:], in_=d_ps[:], func=ACT.Sqrt, scale=0.5, bias=eps_half[:])
+        style_ps = {}
+        d_ps = {}
 
-        def head_recip():
-            nc.vector.reciprocal(out=dec[:], in_=ds[:])
-            nc.vector.tensor_scalar(out=bg[:], in0=bs[:], scalar1=GAIN, scalar2=None, op0=ALU.mult)
+        def style_product(t):
+            cols = slice(t * P, (t + 1) * P)
+            nc.tensor.matmul_mx(out=style_ps[0][:, t, :], lhsT=style_w_q[:, cols].bitcast(X4), lhsT_scale=style_w_s[:, cols],
+                                rhs=w_q[:].bitcast(X4), rhs_scale=w_s[:], start=True, stop=True)
 
-        heads = {"square": head_square, "demod": head_demod, "recip": head_recip}
-        codes, raw, mod, yps, zrow, zclip, zt_ps, qneg, outs = {}, {}, {}, {}, {}, {}, {}, {}, {}
+        def make_style(h):
+            ns = slice(h * HALF, (h + 1) * HALF)
+            nc.vector.scalar_tensor_tensor(
+                out=style[:, ns, :], in0=style_ps[0][:, :, ns].rearrange("p t n -> p n t"), scalar=1.0 / math.sqrt(LATENT),
+                in1=style_b_sb[:].unsqueeze(1).to_broadcast([P, HALF, PACK]), op0=ALU.mult, op1=ALU.add)
 
-        def op_load(u):
-            x_sb = xpool.tile([P, J, C], BF16, name="x_sb")
-            nc.sync.dma_start(out=x_sb[:].rearrange("p j c -> p (j c)"), in_=xv[u])
-            xs[u] = x_sb
+        def square_style(h):
+            cols = slice(h * HALF * PACK, (h + 1) * HALF * PACK)
+            nc.scalar.activation(out=style2_t[:, cols], in_=style[:].rearrange("p n t -> p (n t)")[:, cols], func=ACT.Square)
 
-        def op_turn(u):
+        def quantise_style2(h):
+            ns = slice(h * HALF, (h + 1) * HALF)
+            nc.vector.quantize_mx(out=style2_q[:, ns].bitcast(X4), scales=style2_s[:, ns],
+                                  in_=style2_t[:, h * HALF * PACK : (h + 1) * HALF * PACK])
+
+        def d_product(h):
+            ns = slice(h * HALF, (h + 1) * HALF)
+            d_ps[h] = z_ps.tile([P, PACK, HALF], F32, name="zt")
+            for k in range(PACK):
+                cols = slice(k * P, (k + 1) * P)
+                nc.tensor.matmul_mx(out=d_ps[h][:, k, :], lhsT=weight2_q[:, cols].bitcast(X4), lhsT_scale=weight2_s[:, cols],
+                                    rhs=style2_q[:, ns].bitcast(X4), rhs_scale=style2_s[:, ns], start=True, stop=True)
+
+        def take_root(h):
+            ns = slice(h * HALF, (h + 1) * HALF)
+            nc.scalar.activation(out=root[:, :, ns], in_=d_ps[h][:], func=ACT.Sqrt, scale=0.5, bias=half_eps[:])
+
+        def take_reciprocal(h):
+            ns = slice(h * HALF, (h + 1) * HALF)
+            nc.vector.reciprocal(out=decoef[:, :, ns], in_=root[:, :, ns])
+
+        turned_x, modulated, quantised, products, z, clipped, steep, turned_z, relu, finished = ({} for d in range(10))
+
+        def turn(u):
             xt = xt_ps.tile([P, J, 2, P], F32, name="xt")
-            x_sb = xs.pop(u)
+            x_sb = x_tiles.pop(u)
             for j in range(J):
-                transpose_words(xt[:, j], x_sb[:, j, :].bitcast(F32))
-            raw[u] = xt
+                transpose_words(xt[:, j], x_sb[:, j, :])
+            turned_x[u] = xt
 
-        def op_mod(u, j):
+        def modulate(u, j):
             if j == 0:
-                mod[u] = work.tile([P, J, P, T], BF16, name="xm", align_bytes=64)
-            st = style[:, u * NU : (u + 1) * NU, :].rearrange("p n (u e) -> p n u e", e=2)
+                modulated[u] = work.tile([P, J, P, PACK], BF16, name="xm", align_bytes=64)
+            of_group = style[:, u * GROUP_SAMPLES : (u + 1) * GROUP_SAMPLES, :].rearrange("p n (u e) -> p n u e", e=2)
             nc.vector.tensor_tensor(
-                out=mod[u][:, j].rearrange("p (n l) (u e) -> p n l u e", n=NU, e=2),
-                in0=raw[u][:, j].bitcast(BF16).rearrange("p u (n l e) -> p n l u e", n=NU, e=2),
-                in1=st.unsqueeze(2).to_broadcast([P, NU, LG, 2, 2]),
+                out=modulated[u][:, j].rearrange("p (n l) (u e) -> p n l u e", n=GROUP_SAMPLES, e=2),
+                in0=turned_x[u][:, j].bitcast(BF16).rearrange("p u (n l e) -> p n l u e", n=GROUP_SAMPLES, e=2),
+                in1=of_group.unsqueeze(2).to_broadcast([P, GROUP_SAMPLES, ROWS, 2, 2]),
                 op=ALU.mult)
 
-        def op_quant(u):
-            xq = work.tile([P, TOK], U32, name="xq", align_bytes=64)
-            xqs = work.tile([P, TOK], U8, name="xqs", align_bytes=64)
-            nc.vector.quantize_mx(out=xq[:].bitcast(X4), scales=xqs[:],
-                                  in_=mod.pop(u)[:].rearrange("p j r t -> p (j r t)"))
-            codes[u] = (xq, xqs)
+        def quantise(u):
+            codes = work.tile([P, TOKENS], U32, name="xq", align_bytes=64)
+            scales = work.tile([P, TOKENS], U8, name="xs", align_bytes=64)
+            nc.vector.quantize_mx(out=codes[:].bitcast(X4), scales=scales[:],
+                                  in_=modulated.pop(u)[:].rearrange("p j r t -> p (j r t)"))
+            quantised[u] = (codes, scales)
 
-        def op_mm(u, h):
-            xq, xqs = codes[u]
-            yt = y_ps.tile([P, 2, TOK], F32, name="yt")
-            for kk in DUP:
-                cs = slice((2 * h + kk) * P, (2 * h + kk + 1) * P)
-                nc.tensor.matmul_mx(out=yt[:, kk, :], lhsT=wtq[:, cs].bitcast(X4), lhsT_scale=wts[:, cs],
-                                    rhs=xq[:].bitcast(X4), rhs_scale=xqs[:], start=True, stop=True)
-            yps[u, h] = yt
+        def product(u, h):
+            codes, scales = quantised[u]
+            yt = y_ps.tile([P, 2, TOKENS], F32, name="yt")
+            for part in range(2):
+                cols = slice((2 * h + part) * P, (2 * h + part + 1) * P)
+                nc.tensor.matmul_mx(out=yt[:, part, :], lhsT=weight_q[:, cols].bitcast(X4), lhsT_scale=weight_s[:, cols],
+                                    rhs=codes[:].bitcast(X4), rhs_scale=scales[:], start=True, stop=True)
+            products[u, h] = yt
 
-        def op_affine(u, h):
+        def demodulate(u, h):
             if h == 0:
-                zrow[u] = work.tile([P, T, TOK], F32, name="zr")
-            yt = yps.pop((u, h))
-            for kk in range(2):
-                k = 2 * h + kk
-                for n in range(NU):
-                    s = u * NU + n
+                z[u] = work.tile([P, PACK, TOKENS], F32, name="zr")
+            yt = products.pop((u, h))
+            for part in range(2):
+                k = 2 * h + part
+                for n in range(GROUP_SAMPLES):
+                    sample = u * GROUP_SAMPLES + n
                     nc.scalar.activation(
-                        out=zrow[u][:, k, :].rearrange("p (j n l) -> p n j l", j=J, n=NU)[:, n],
-                        in_=yt[:, kk, :].rearrange("p (j n l) -> p n j l", j=J, n=NU)[:, n],
-                        func=ACT.Identity, scale=dec[:, k, s : s + 1], bias=bg[:, k : k + 1])
+                        out=z[u][:, k, :].rearrange("p (j n l) -> p n j l", j=J, n=GROUP_SAMPLES)[:, n],
+                        in_=yt[:, part, :].rearrange("p (j n l) -> p n j l", j=J, n=GROUP_SAMPLES)[:, n],
+                        func=ACT.Identity, scale=decoef[:, k, sample : sample + 1], bias=bias_gain[:, k : k + 1])
 
-        def op_clip(u, h):
+        def clip(u, h):
             if h == 0:
-                zclip[u] = work.tile([P, T, TOK], F32, name="zc")
+                clipped[u] = work.tile([P, PACK, TOKENS], F32, name="zc")
             ks = slice(2 * h, 2 * h + 2)
-            nc.gpsimd.tensor_scalar(out=zclip[u][:, ks, :], in0=zrow[u][:, ks, :], scalar1=CLAMP,
+            cols = slice(0, sum((u, j) not in SUMMED for j in range(J)) * P)
+            nc.gpsimd.tensor_scalar(out=clipped[u][:, ks, cols], in0=z[u][:, ks, cols], scalar1=CLAMP,
                                     scalar2=-CLAMP / SLOPE, op0=ALU.min, op1=ALU.max)
 
-        def op_back(u, j):
-            zt = z_ps.tile([P, T, P], F32, name="zt")
-            for k in range(T):
-                nc.tensor.transpose(zt[:, k, :], zclip[u][:, k, j * P : (j + 1) * P], ident[:])
-            zt_ps[u, j] = zt
+        def make_steep(u):
+            for j in range(J):
+                if (u, j) in SUMMED:
+                    negative = work.tile([P, PACK, P], F32, name="nq")
+                    nc.gpsimd.tensor_scalar(out=negative[:], in0=z[u][:, :, j * P : (j + 1) * P], scalar1=0.0,
+                                            scalar2=-CLAMP / SLOPE, op0=ALU.min, op1=ALU.max)
+                    steep[u, j] = work.tile([P, PACK, P], F32, name="q")
+                    nc.gpsimd.tensor_scalar(out=steep[u, j][:], in0=negative[:], scalar1=-(1.0 - SLOPE), scalar2=1.0,
+                                            op0=ALU.mult, op1=ALU.mult)
 
-        def op_neg(u, j):
-            qn = work.tile([P, P, T], F32, name="qn")
-            nc.scalar.activation(out=qn[:], in_=zt_ps[u, j][:].rearrange("p k m -> p m k"), func=ACT.Relu,
-                                 scale=-(1.0 - SLOPE))
-            qneg[u, j] = qn
+        def turn_back(u, j):
+            zt = z_ps.tile([P, PACK, P], F32, name="zt")
+            summed = (u, j) in SUMMED
+            source = z[u] if summed else clipped[u]
+            for k in range(PACK):
+                as_product = (j, k) == IDENTITY_PRODUCT and u < IDENTITY_PRODUCT_GROUPS
+                nc.tensor.matmul(out=zt[:, k, :], lhsT=source[:, k, j * P : (j + 1) * P], rhs=ident[:],
+                                 is_transpose=not as_product, start=True, stop=not summed)
+                if summed:
+                    nc.tensor.matmul(out=zt[:, k, :], lhsT=steep[u, j][:, k, :], rhs=ident[:],
+                                     is_transpose=True, start=False, stop=True)
+            turned_z[u, j] = zt
 
-        def op_out(u, j):
+        def make_relu(u, j):
+            if (u, j) in SUMMED:
+                return
+            relu[u, j] = work.tile([P, P, PACK], F32, name="qn")
+            in_order = turned_z[u, j][:].rearrange("p k m -> p m k")
+            if (u, j) in VECTOR_RELU:
+                nc.vector.tensor_scalar(out=relu[u, j][:], in0=in_order, scalar1=0.0, scalar2=-(1.0 - SLOPE),
+                                        op0=ALU.min, op1=ALU.mult)
+            else:
+                nc.scalar.activation(out=relu[u, j][:], in_=in_order, func=ACT.Relu, scale=-(1.0 - SLOPE))
+
+        def finish(u, j):
             if j == 0:
-                outs[u] = work.tile([P, J, O], F32, name="ot")
-            nc.vector.tensor_tensor(out=outs[u][:, j, :].rearrange("p (m k) -> p m k", k=T),
-                                    in0=zt_ps[u, j][:].rearrange("p k m -> p m k"), in1=qneg[u, j][:], op=ALU.add)
+                finished[u] = work.tile([P, J, O], F32, name="ot")
+            row = finished[u][:, j, :].rearrange("p (m k) -> p m k", k=PACK)
+            in_order = turned_z[u, j][:].rearrange("p k m -> p m k")
+            if (u, j) in SUMMED:
+                nc.vector.tensor_scalar(out=row, in0=in_order, scalar1=CLAMP, scalar2=-CLAMP, op0=ALU.min, op1=ALU.max)
+            else:
+                nc.vector.tensor_tensor(out=row, in0=in_order, in1=relu[u, j][:], op=ALU.add)
 
-        def op_store(u):
-            nc.sync.dma_start(out=ov[u], in_=outs[u][:].rearrange("p j o -> p (j o)"))
+        def store(u):
+            if u < GROUPS - 1:
+                nc.sync.dma_start(out=out_view[u], in_=finished[u][:].rearrange("p j o -> p (j o)"))
+            else:
+                for j in range(J):
+                    nc.sync.dma_start(out=out_view[u].rearrange("p (j o) -> p j o", j=J)[:, j, :], in_=finished[u][:, j, :])
 
-        ops = {"L": op_load, "T": op_turn, "Q": op_quant, "ST": op_store,
-               "P0": lambda u: op_mod(u, 0), "P1": lambda u: op_mod(u, 1),
-               "M0": lambda u: op_mm(u, 0), "M1": lambda u: op_mm(u, 1),
-               "A0": lambda u: op_affine(u, 0), "A1": lambda u: op_affine(u, 1),
-               "C0": lambda u: op_clip(u, 0), "C1": lambda u: op_clip(u, 1),
-               "B0": lambda u: op_back(u, 0), "B1": lambda u: op_back(u, 1),
-               "R0": lambda u: op_neg(u, 0), "R1": lambda u: op_neg(u, 1),
-               "F0": lambda u: op_out(u, 0), "F1": lambda u: op_out(u, 1)}
-        first = -max(o for name, o in PIPE if name != "L")
-        for i in range(first, UNITS + 8):
-            for name, o in PIPE:
-                for what, hi, hname in HEAD_AT:
-                    if (i, name) == (hi, hname):
-                        heads[what]()
-                u = i + o
-                if 0 <= u < UNITS and not (name == "L" and u < LOADED):
-                    ops[name](u)
+        warm(6)
+        nc.vector.tensor_copy(out=w_bf[:], in_=w_codes[:].bitcast(FP8))
+        style_w_ps = [turn_rows(y_ps, "yt", style_w_sb, 0)]
+        w_ps = y_ps.tile([P, 2, P], F32, name="yt")
+        transpose_words(w_ps[:], w_bf[:])
+        nc.vector.tensor_tensor(
+            out=w_t[:].rearrange("p n (u e) -> p n u e", e=2),
+            in0=w_ps[:].bitcast(BF16).rearrange("p u (n e) -> p n u e", e=2),
+            in1=w_scale_sb[:].rearrange("p (u e) -> p u e", e=2).unsqueeze(1).to_broadcast([P, SAMPLES, 2, 2]),
+            op=ALU.mult)
+        style_w_ps.append(turn_rows(y_ps, "yt", style_w_sb, 1))
+        for h in range(2):
+            nc.scalar.copy(out=halves(style_w_t, h), in_=style_w_ps[h][:].rearrange("p t u m -> p t m u"))
+        nc.vector.quantize_mx(out=w_q[:].bitcast(X4), scales=w_s[:], in_=w_t[:].rearrange("p n k -> p (n k)"))
+        for h in range(2):
+            quantise_style_w(h)
+        weight_ps = [turn_rows(z_ps, "zt", weight_sb, h) for h in range(2)]
+        style_ps[0] = z_ps.tile([P, PACK, P], F32, name="zt")
+        for t in range(PACK):
+            style_product(t)
+        nc.vector.tensor_copy(out=halves(weight_t, 1), in_=weight_ps[1][:].rearrange("p t u m -> p t m u"))
+        turn(0)
+        nc.vector.tensor_scalar(out=bias_gain[:], in0=bias_sb[:], scalar1=GAIN, scalar2=None, op0=ALU.mult)
+        square_on_vector(1)
+        turn(1)
+        make_style(0)
+        nc.scalar.copy(out=halves(weight_t, 0), in_=weight_ps[0][:].rearrange("p t u m -> p t m u"))
+        square_on_scalar(0)
+        warm_mx(1)
+        square_style(0)
+        nc.vector.quantize_mx(out=weight2_q[:].bitcast(X4), scales=weight2_s[:], in_=weight2_t[:])
+        quantise_style2(0)
+        d_product(0)
+        modulate(0, 0)
+        nc.vector.quantize_mx(out=weight_q[:].bitcast(X4), scales=weight_s[:], in_=weight_flat)
+        modulate(1, 0)
+        take_root(0)
+        take_reciprocal(0)
+        warm_mx(5)
+
+        steps = {"load": load, "turn": turn, "quantise": quantise, "steep": make_steep, "store": store}
+        for name, step in (("modulate", modulate), ("product", product), ("demodulate", demodulate), ("clip", clip),
+                           ("back", turn_back), ("relu", make_relu), ("finish", finish)):
+            for part in range(2):
+                steps["%s %d" % (name, part)] = lambda u, step=step, part=part: step(u, part)
+        second_half = {"style": make_style, "square": square_style, "quantise": quantise_style2, "product": d_product,
+                       "root": take_root, "reciprocal": take_reciprocal}
+
+        for i in range(FIRST_TURN, GROUPS + 2):
+            for name, ahead in STEPS:
+                if (i, name) in SECOND_HALF:
+                    second_half[SECOND_HALF[i, name]](1)
+                u = i + ahead
+                if 0 <= u < GROUPS and (name, u) not in EARLY:
+                    steps[name](u)

import math
from contextlib import ExitStack

import concourse.mybir as mybir
from concourse.masks import make_identity

SAMPLES, POINTS, LATENT, C, O = 128, 64, 512, 512, 512
EPS = 1e-8
CLAMP = 256.0
SLOPE = 0.2
GAIN = math.sqrt(2.0)
FLOPS = 2 * SAMPLES * POINTS * C * O + 2 * SAMPLES * LATENT * C + 2 * SAMPLES * C * O

F32 = mybir.dt.float32
BF16 = mybir.dt.bfloat16
U32 = mybir.dt.uint32
U8 = mybir.dt.uint8
FP8 = mybir.dt.float8_e4m3fn
X4 = mybir.dt.float8_e4m3fn_x4
ALU = mybir.AluOpType
ACT = mybir.ActivationFunctionType

P = 128
PACK = 4
GROUP_SAMPLES = 4
TOKENS = GROUP_SAMPLES * POINTS
J = TOKENS // P
ROWS = POINTS // J
GROUPS = SAMPLES // GROUP_SAMPLES
HALF = SAMPLES // 2
PRELOADED = 8
X_TILES = PRELOADED + 2

SUMMED = {(u, 1) for u in range(0, GROUPS - 2, 2)} | {(GROUPS - 3, 1)}
VECTOR_RELU = {(GROUPS - 3, 0)}

IDENTITY_PRODUCT = (0, PACK - 1)
IDENTITY_PRODUCT_GROUPS = GROUPS - 2

STEPS = (
    ("load", PRELOADED),
    ("back 0", -2),
    ("modulate 0", 3),
    ("demodulate 0", 0),
    ("quantise", 2),
    ("product 1", 0),
    ("relu 0", -2),
    ("demodulate 1", 0),
    ("clip 0", 0),
    ("finish 0", -2),
    ("product 0", 1),
    ("clip 1", 0),
    ("back 1", -2),
    ("steep", 0),
    ("relu 1", -2),
    ("modulate 1", 3),
    ("turn", 4),
    ("finish 1", -2),
    ("store", -2),
)
FIRST_TURN = -4
EARLY = {("turn", 0), ("turn", 1), ("modulate 0", 0), ("modulate 0", 1)} | {("load", u) for u in range(PRELOADED)}
SECOND_HALF = {
    (-2, "quantise"): "style",
    (-2, "steep"): "square",
    (-1, "product 1"): "quantise",
    (0, "back 1"): "product",
    (2, "clip 0"): "root",
    (3, "steep"): "reciprocal",
}


def tile_modulatemlp_pa_kernel(tc, x, w_bytes, w_scale, weight, style_w, style_b, bias, out):
    nc = tc.nc
    x_view = x.rearrange("n l c -> (n l) c").rearrange("(g r j) c -> g r (j c)", r=P, j=J)
    out_view = out.rearrange("n l o -> (n l) o").rearrange("(g r j) o -> g r (j o)", r=P, j=J)

    with ExitStack() as ctx:
        ctx.enter_context(tc.manual_schedule())
        keep = ctx.enter_context(tc.tile_pool(name="keep", bufs=1))
        x_pool = ctx.enter_context(tc.tile_pool(name="x_pool", bufs=X_TILES))
        work = ctx.enter_context(tc.tile_pool(name="work", bufs=4))
        xt_ps = ctx.enter_context(tc.psum_pool(name="xt_ps", bufs=2))
        y_ps = ctx.enter_context(tc.psum_pool(name="y_ps", bufs=3))
        z_ps = ctx.enter_context(tc.psum_pool(name="z_ps", bufs=3))

        style_w_sb = keep.tile([P, PACK, LATENT], BF16)
        weight_sb = keep.tile([P, PACK, C], BF16)
        w_codes = keep.tile([P, LATENT], U8)
        w_scale_sb = keep.tile([P, PACK], F32)
        style_b_sb = keep.tile([P, PACK], BF16)
        bias_sb = keep.tile([P, PACK], BF16)
        style_w_view = style_w.rearrange("(m t) l -> m t l", t=PACK)
        nc.sync.dma_start(out=w_codes[:], in_=w_bytes)
        nc.sync.dma_start(out=style_w_sb[:, 0:2, :], in_=style_w_view[:, 0:2, :])
        nc.sync.dma_start(out=style_w_sb[:, 2:4, :], in_=style_w_view[:, 2:4, :])
        nc.scalar.dma_start(out=w_scale_sb[:], in_=w_scale.rearrange("o (p t) -> p (o t)", t=PACK))
        nc.scalar.dma_start(out=style_b_sb[:], in_=style_b.rearrange("(p t) -> p t", t=PACK))
        nc.scalar.dma_start(out=bias_sb[:], in_=bias.rearrange("(p t) -> p t", t=PACK))
        nc.sync.dma_start(out=weight_sb[:], in_=weight.rearrange("(m k) c -> m k c", k=PACK))

        x_tiles = {}

        def load(u):
            x_sb = x_pool.tile([P, J, C], BF16, name="x_sb")
            nc.sync.dma_start(out=x_sb[:].rearrange("p j c -> p (j c)"), in_=x_view[u])
            x_tiles[u] = x_sb

        for u in range(PRELOADED):
            load(u)

        ident = keep.tile([P, P], F32)
        make_identity(nc, ident[:])
        ones = keep.tile([P, 1], F32)
        nc.vector.memset(ones[:], 1.0)
        table_out = keep.tile([P, 1], F32)
        nc.scalar.activation(out=table_out[:], in_=ones[:], func=ACT.Sqrt)
        zero = keep.tile([P, 512], BF16)
        nc.vector.memset(zero[:], 0.0)
        half_eps = keep.tile([P, 1], F32)
        nc.vector.tensor_scalar(out=half_eps[:], in0=ones[:], scalar1=0.5 * EPS, scalar2=None, op0=ALU.mult)

        style_w_q = keep.tile([P, C], U32, align_bytes=64)
        style_w_s = keep.tile([P, C], U8, align_bytes=64)
        w_q = keep.tile([P, SAMPLES], U32, align_bytes=64)
        w_s = keep.tile([P, SAMPLES], U8, align_bytes=64)
        weight_q = keep.tile([P, O], U32, align_bytes=64)
        weight_s = keep.tile([P, O], U8, align_bytes=64)
        weight2_q = keep.tile([P, O], U32, align_bytes=64)
        weight2_s = keep.tile([P, O], U8, align_bytes=64)
        style2_q = keep.tile([P, SAMPLES], U32, align_bytes=64)
        style2_s = keep.tile([P, SAMPLES], U8, align_bytes=64)
        style_w_t = keep.tile([P, PACK, P, PACK], BF16, align_bytes=64)
        w_t = keep.tile([P, SAMPLES, PACK], BF16, align_bytes=64)
        weight_t = keep.tile([P, PACK, P, PACK], BF16, align_bytes=64)
        weight2_t = keep.tile([P, O * PACK], BF16, align_bytes=64)
        style2_t = keep.tile([P, SAMPLES * PACK], BF16, align_bytes=64)
        weight_flat = weight_t[:].rearrange("p k m c -> p (k m c)")
        w_bf = keep.tile([P, LATENT], BF16)
        style = keep.tile([P, SAMPLES, PACK], F32)
        root = keep.tile([P, PACK, SAMPLES], F32)
        decoef = keep.tile([P, PACK, SAMPLES], F32)
        bias_gain = keep.tile([P, PACK], F32)

        def transpose_words(dst, row):
            words = row.bitcast(F32)
            for h in range(2):
                nc.tensor.transpose(dst[:, h, :], words[:, h::2], ident[:])

        def halves(big, h):
            part = big[:, 2 * h : 2 * h + 2].rearrange("p t m k -> p t (m k)").bitcast(F32)
            return part.rearrange("p t (m u) -> p t m u", u=2)

        def warm(count):
            unused = xt_ps.tile([P, J, 2, P], F32, name="xt")
            for r in range(count):
                nc.tensor.matmul(out=unused[:].rearrange("p j u r -> p (j u r)"), lhsT=zero[:, :P], rhs=zero[:],
                                 start=True, stop=True)

        def warm_mx(count):
            unused = y_ps.tile([P, 2, TOKENS], F32, name="yt")
            for r in range(count):
                nc.tensor.matmul_mx(out=unused[:].rearrange("p j u -> p (j u)"), lhsT=style_w_q[:, :P].bitcast(X4),
                                    lhsT_scale=style_w_s[:, :P], rhs=style_w_q[:].bitcast(X4),
                                    rhs_scale=style_w_s[:], start=True, stop=True)

        def turn_rows(pool, name, rows, h):
            turned = pool.tile([P, 2, 2, P], F32, name=name)
            for k in range(2):
                transpose_words(turned[:, k], rows[:, 2 * h + k, :])
            return turned

        def quantise_style_w(h):
            cols = slice(2 * P * h, 2 * P * (h + 1))
            nc.vector.quantize_mx(out=style_w_q[:, cols].bitcast(X4), scales=style_w_s[:, cols],
                                  in_=style_w_t[:, 2 * h : 2 * h + 2].rearrange("p t m k -> p (t m k)"))

        def square_on_scalar(h):
            cols = slice(h * 2 * P * PACK, (h + 1) * 2 * P * PACK)
            nc.scalar.activation(out=weight2_t[:, cols], in_=weight_flat[:, cols], func=ACT.Square)

        def square_on_vector(h):
            cols = slice(h * 2 * P * PACK, (h + 1) * 2 * P * PACK)
            nc.vector.tensor_tensor(out=weight2_t[:, cols], in0=weight_flat[:, cols], in1=weight_flat[:, cols], op=ALU.mult)

        style_ps = {}
        d_ps = {}

        def style_product(t):
            cols = slice(t * P, (t + 1) * P)
            nc.tensor.matmul_mx(out=style_ps[0][:, t, :], lhsT=style_w_q[:, cols].bitcast(X4), lhsT_scale=style_w_s[:, cols],
                                rhs=w_q[:].bitcast(X4), rhs_scale=w_s[:], start=True, stop=True)

        def make_style(h):
            ns = slice(h * HALF, (h + 1) * HALF)
            nc.vector.scalar_tensor_tensor(
                out=style[:, ns, :], in0=style_ps[0][:, :, ns].rearrange("p t n -> p n t"), scalar=1.0 / math.sqrt(LATENT),
                in1=style_b_sb[:].unsqueeze(1).to_broadcast([P, HALF, PACK]), op0=ALU.mult, op1=ALU.add)

        def square_style(h):
            cols = slice(h * HALF * PACK, (h + 1) * HALF * PACK)
            nc.scalar.activation(out=style2_t[:, cols], in_=style[:].rearrange("p n t -> p (n t)")[:, cols], func=ACT.Square)

        def quantise_style2(h):
            ns = slice(h * HALF, (h + 1) * HALF)
            nc.vector.quantize_mx(out=style2_q[:, ns].bitcast(X4), scales=style2_s[:, ns],
                                  in_=style2_t[:, h * HALF * PACK : (h + 1) * HALF * PACK])

        def d_product(h):
            ns = slice(h * HALF, (h + 1) * HALF)
            d_ps[h] = z_ps.tile([P, PACK, HALF], F32, name="zt")
            for k in range(PACK):
                cols = slice(k * P, (k + 1) * P)
                nc.tensor.matmul_mx(out=d_ps[h][:, k, :], lhsT=weight2_q[:, cols].bitcast(X4), lhsT_scale=weight2_s[:, cols],
                                    rhs=style2_q[:, ns].bitcast(X4), rhs_scale=style2_s[:, ns], start=True, stop=True)

        def take_root(h):
            ns = slice(h * HALF, (h + 1) * HALF)
            nc.scalar.activation(out=root[:, :, ns], in_=d_ps[h][:], func=ACT.Sqrt, scale=0.5, bias=half_eps[:])

        def take_reciprocal(h):
            ns = slice(h * HALF, (h + 1) * HALF)
            nc.vector.reciprocal(out=decoef[:, :, ns], in_=root[:, :, ns])

        turned_x, modulated, quantised, products, z, clipped, steep, turned_z, relu, finished = ({} for d in range(10))

        def turn(u):
            xt = xt_ps.tile([P, J, 2, P], F32, name="xt")
            x_sb = x_tiles.pop(u)
            for j in range(J):
                transpose_words(xt[:, j], x_sb[:, j, :])
            turned_x[u] = xt

        def modulate(u, j):
            if j == 0:
                modulated[u] = work.tile([P, J, P, PACK], BF16, name="xm", align_bytes=64)
            of_group = style[:, u * GROUP_SAMPLES : (u + 1) * GROUP_SAMPLES, :].rearrange("p n (u e) -> p n u e", e=2)
            nc.vector.tensor_tensor(
                out=modulated[u][:, j].rearrange("p (n l) (u e) -> p n l u e", n=GROUP_SAMPLES, e=2),
                in0=turned_x[u][:, j].bitcast(BF16).rearrange("p u (n l e) -> p n l u e", n=GROUP_SAMPLES, e=2),
                in1=of_group.unsqueeze(2).to_broadcast([P, GROUP_SAMPLES, ROWS, 2, 2]),
                op=ALU.mult)

        def quantise(u):
            codes = work.tile([P, TOKENS], U32, name="xq", align_bytes=64)
            scales = work.tile([P, TOKENS], U8, name="xs", align_bytes=64)
            nc.vector.quantize_mx(out=codes[:].bitcast(X4), scales=scales[:],
                                  in_=modulated.pop(u)[:].rearrange("p j r t -> p (j r t)"))
            quantised[u] = (codes, scales)

        def product(u, h):
            codes, scales = quantised[u]
            yt = y_ps.tile([P, 2, TOKENS], F32, name="yt")
            for part in range(2):
                cols = slice((2 * h + part) * P, (2 * h + part + 1) * P)
                nc.tensor.matmul_mx(out=yt[:, part, :], lhsT=weight_q[:, cols].bitcast(X4), lhsT_scale=weight_s[:, cols],
                                    rhs=codes[:].bitcast(X4), rhs_scale=scales[:], start=True, stop=True)
            products[u, h] = yt

        def demodulate(u, h):
            if h == 0:
                z[u] = work.tile([P, PACK, TOKENS], F32, name="zr")
            yt = products.pop((u, h))
            for part in range(2):
                k = 2 * h + part
                for n in range(GROUP_SAMPLES):
                    sample = u * GROUP_SAMPLES + n
                    nc.scalar.activation(
                        out=z[u][:, k, :].rearrange("p (j n l) -> p n j l", j=J, n=GROUP_SAMPLES)[:, n],
                        in_=yt[:, part, :].rearrange("p (j n l) -> p n j l", j=J, n=GROUP_SAMPLES)[:, n],
                        func=ACT.Identity, scale=decoef[:, k, sample : sample + 1], bias=bias_gain[:, k : k + 1])

        def clip(u, h):
            if h == 0:
                clipped[u] = work.tile([P, PACK, TOKENS], F32, name="zc")
            ks = slice(2 * h, 2 * h + 2)
            cols = slice(0, sum((u, j) not in SUMMED for j in range(J)) * P)
            nc.gpsimd.tensor_scalar(out=clipped[u][:, ks, cols], in0=z[u][:, ks, cols], scalar1=CLAMP,
                                    scalar2=-CLAMP / SLOPE, op0=ALU.min, op1=ALU.max)

        def make_steep(u):
            for j in range(J):
                if (u, j) in SUMMED:
                    negative = work.tile([P, PACK, P], F32, name="nq")
                    nc.gpsimd.tensor_scalar(out=negative[:], in0=z[u][:, :, j * P : (j + 1) * P], scalar1=0.0,
                                            scalar2=-CLAMP / SLOPE, op0=ALU.min, op1=ALU.max)
                    steep[u, j] = work.tile([P, PACK, P], F32, name="q")
                    nc.gpsimd.tensor_scalar(out=steep[u, j][:], in0=negative[:], scalar1=-(1.0 - SLOPE), scalar2=1.0,
                                            op0=ALU.mult, op1=ALU.mult)

        def turn_back(u, j):
            zt = z_ps.tile([P, PACK, P], F32, name="zt")
            summed = (u, j) in SUMMED
            source = z[u] if summed else clipped[u]
            for k in range(PACK):
                as_product = (j, k) == IDENTITY_PRODUCT and u < IDENTITY_PRODUCT_GROUPS
                nc.tensor.matmul(out=zt[:, k, :], lhsT=source[:, k, j * P : (j + 1) * P], rhs=ident[:],
                                 is_transpose=not as_product, start=True, stop=not summed)
                if summed:
                    nc.tensor.matmul(out=zt[:, k, :], lhsT=steep[u, j][:, k, :], rhs=ident[:],
                                     is_transpose=True, start=False, stop=True)
            turned_z[u, j] = zt

        def make_relu(u, j):
            if (u, j) in SUMMED:
                return
            relu[u, j] = work.tile([P, P, PACK], F32, name="qn")
            in_order = turned_z[u, j][:].rearrange("p k m -> p m k")
            if (u, j) in VECTOR_RELU:
                nc.vector.tensor_scalar(out=relu[u, j][:], in0=in_order, scalar1=0.0, scalar2=-(1.0 - SLOPE),
                                        op0=ALU.min, op1=ALU.mult)
            else:
                nc.scalar.activation(out=relu[u, j][:], in_=in_order, func=ACT.Relu, scale=-(1.0 - SLOPE))

        def finish(u, j):
            if j == 0:
                finished[u] = work.tile([P, J, O], F32, name="ot")
            row = finished[u][:, j, :].rearrange("p (m k) -> p m k", k=PACK)
            in_order = turned_z[u, j][:].rearrange("p k m -> p m k")
            if (u, j) in SUMMED:
                nc.vector.tensor_scalar(out=row, in0=in_order, scalar1=CLAMP, scalar2=-CLAMP, op0=ALU.min, op1=ALU.max)
            else:
                nc.vector.tensor_tensor(out=row, in0=in_order, in1=relu[u, j][:], op=ALU.add)

        def store(u):
            if u < GROUPS - 1:
                nc.sync.dma_start(out=out_view[u], in_=finished[u][:].rearrange("p j o -> p (j o)"))
            else:
                for j in range(J):
                    nc.sync.dma_start(out=out_view[u].rearrange("p (j o) -> p j o", j=J)[:, j, :], in_=finished[u][:, j, :])

        warm(6)
        nc.vector.tensor_copy(out=w_bf[:], in_=w_codes[:].bitcast(FP8))
        style_w_ps = [turn_rows(y_ps, "yt", style_w_sb, 0)]
        w_ps = y_ps.tile([P, 2, P], F32, name="yt")
        transpose_words(w_ps[:], w_bf[:])
        nc.vector.tensor_tensor(
            out=w_t[:].rearrange("p n (u e) -> p n u e", e=2),
            in0=w_ps[:].bitcast(BF16).rearrange("p u (n e) -> p n u e", e=2),
            in1=w_scale_sb[:].rearrange("p (u e) -> p u e", e=2).unsqueeze(1).to_broadcast([P, SAMPLES, 2, 2]),
            op=ALU.mult)
        style_w_ps.append(turn_rows(y_ps, "yt", style_w_sb, 1))
        for h in range(2):
            nc.scalar.copy(out=halves(style_w_t, h), in_=style_w_ps[h][:].rearrange("p t u m -> p t m u"))
        nc.vector.quantize_mx(out=w_q[:].bitcast(X4), scales=w_s[:], in_=w_t[:].rearrange("p n k -> p (n k)"))
        for h in range(2):
            quantise_style_w(h)
        weight_ps = [turn_rows(z_ps, "zt", weight_sb, h) for h in range(2)]
        style_ps[0] = z_ps.tile([P, PACK, P], F32, name="zt")
        for t in range(PACK):
            style_product(t)
        nc.vector.tensor_copy(out=halves(weight_t, 1), in_=weight_ps[1][:].rearrange("p t u m -> p t m u"))
        turn(0)
        nc.vector.tensor_scalar(out=bias_gain[:], in0=bias_sb[:], scalar1=GAIN, scalar2=None, op0=ALU.mult)
        square_on_vector(1)
        turn(1)
        make_style(0)
        nc.scalar.copy(out=halves(weight_t, 0), in_=weight_ps[0][:].rearrange("p t u m -> p t m u"))
        square_on_scalar(0)
        warm_mx(1)
        square_style(0)
        nc.vector.quantize_mx(out=weight2_q[:].bitcast(X4), scales=weight2_s[:], in_=weight2_t[:])
        quantise_style2(0)
        d_product(0)
        modulate(0, 0)
        nc.vector.quantize_mx(out=weight_q[:].bitcast(X4), scales=weight_s[:], in_=weight_flat)
        modulate(1, 0)
        take_root(0)
        take_reciprocal(0)
        warm_mx(5)

        steps = {"load": load, "turn": turn, "quantise": quantise, "steep": make_steep, "store": store}
        for name, step in (("modulate", modulate), ("product", product), ("demodulate", demodulate), ("clip", clip),
                           ("back", turn_back), ("relu", make_relu), ("finish", finish)):
            for part in range(2):
                steps["%s %d" % (name, part)] = lambda u, step=step, part=part: step(u, part)
        second_half = {"style": make_style, "square": square_style, "quantise": quantise_style2, "product": d_product,
                       "root": take_root, "reciprocal": take_reciprocal}

        for i in range(FIRST_TURN, GROUPS + 2):
            for name, ahead in STEPS:
                if (i, name) in SECOND_HALF:
                    second_half[SECOND_HALF[i, name]](1)
                u = i + ahead
                if 0 <= u < GROUPS and (name, u) not in EARLY:
                    steps[name](u)
